import numpy as np
import ml_dtypes


def mxq(x, axis, fmt="e4m3"):
    dtype, down = {"e4m3": (ml_dtypes.float8_e4m3fn, 7), "e5m2": (ml_dtypes.float8_e5m2, 14)}[fmt]
    v = np.moveaxis(np.asarray(x, np.float32).astype(ml_dtypes.bfloat16).astype(np.float64), axis, -1)
    blocks = v.reshape(v.shape[:-1] + (-1, 32))
    amax = np.abs(blocks).max(-1, keepdims=True)
    byte = np.maximum(np.where(amax > 0, np.frexp(amax)[1] - 1 + 127, 0) - down, 1)
    scale = np.exp2(byte - 127.0)
    codes = (blocks / scale).astype(np.float32).astype(dtype).astype(np.float64)
    return np.moveaxis((codes * scale).reshape(v.shape), -1, axis)


WIDE = False


def mx_kscale(k):
    if not WIDE:
        return np.ones(k)
    levels = np.array([10, -10, 5, -5, 0])
    a = np.random.permutation(np.resize(levels, k // 512 * 4)).reshape(k // 512, 4)
    idx = np.arange(k)
    return np.exp2(a[idx // 512, idx % 128 // 32])


BF16 = ml_dtypes.bfloat16


def bf(x):
    return np.asarray(x, np.float32).astype(BF16)


def f64(x):
    return np.asarray(x).astype(np.float64)


B, N, H = 2048, 512, 2048
BETA = 0.99
LOG2PI = np.log(2.0 * np.pi)


def lyap(u):
    return np.sum(u * u, axis=-1, keepdims=True) + 1e-3


def setup_inputs():
    s = mx_kscale(H)
    g = np.exp(0.4 * np.random.standard_normal(B))[:, None]
    col = np.concatenate([np.full(N, 3.0), np.full(N, 0.8)])
    off = np.concatenate([np.zeros(N), np.full(N, -1.5)])
    return {"h": bf(np.tanh(np.random.standard_normal((B, H))) * s),
            "W2": bf(np.random.standard_normal((H, 2 * N)) * col / np.sqrt(H) / s[:, None]),
            "b2": bf(np.random.standard_normal(2 * N) * 0.4 + off),
            "x": bf(np.random.standard_normal((B, N)) * 1.5 * g),
            "y": bf(np.random.standard_normal((B, N))[:, None, :] * 0.7),
            "eps": bf(np.random.standard_normal((B, N))[:, None, :]),
            "Wv": bf(np.random.standard_normal((N, N)) * 0.1 / N)}


def reference(h, W2, b2, x, y, eps, Wv):
    f = (mxq(f64(h), 1, "e4m3") @ mxq(f64(W2), 0, "e4m3")) + f64(b2)
    mu, logvar = f[:, :N], f[:, N:]
    mu = mu[:, None, :]
    var = np.exp(logvar)[:, None, :]
    wvq = mxq(f64(Wv), 0, "e4m3")
    Vx = lyap(mxq(f64(x), 1, "e4m3") @ wvq)[:, None, :]
    Vmu = lyap(mxq(mu, 2, "e4m3") @ wvq)
    bVx = BETA * Vx
    mu_stable = mu * ((bVx - np.maximum(bVx - Vmu, 0.0)) / Vmu)
    fx = mu_stable + np.sqrt(var) * f64(eps)
    q = (f64(y) - mu_stable) ** 2 / var
    logp = -0.5 * (N * LOG2PI + np.sum(np.log(var) + q, axis=-1))
    return fx, logp

@@ -1,0 +1,457 @@
+from contextlib import ExitStack
+import math
+
+import concourse.mybir as mybir
+from concourse.masks import make_identity
+
+F32 = mybir.dt.float32
+BF16 = mybir.dt.bfloat16
+U32 = mybir.dt.uint32
+U8 = mybir.dt.uint8
+FP8X4 = mybir.dt.float8_e4m3fn_x4
+ALU = mybir.AluOpType
+ACT = mybir.ActivationFunctionType
+
+P = 128
+B = 2048
+H = 2048
+N = 512
+NT = B // P
+KP = H // 512
+FLOPS = 2 * B * H * 2 * N + 2 * 2 * B * N * N
+
+T_ON_GPSIMD = False
+S_HALVES = ()
+
+
+def tile_mdn_module_pa_kernel(tc, h, W2, b2, x, y, eps, Wv, out_0, out_1):
+    nc = tc.nc
+    h_v = h.rearrange("(p i) k -> p i k", i=NT)
+    x_v = x.rearrange("(p i) n -> p i n", i=NT)
+    y_v = y.rearrange("(p i) o n -> p i (o n)", i=NT)
+    e_v = eps.rearrange("(p i) o n -> p i (o n)", i=NT)
+    fx_v = out_0.rearrange("(p i) o n -> p i (o n)", i=NT)
+    lp_v = out_1.rearrange("(p i) o -> p (i o)", i=NT)
+
+    with ExitStack() as ctx:
+        keep = ctx.enter_context(tc.tile_pool(name="keep", bufs=1))
+        work = ctx.enter_context(tc.tile_pool(name="work", bufs=2))
+        psum = ctx.enter_context(tc.psum_pool(name="psum", bufs=1))
+        ctx.enter_context(tc.manual_schedule())
+
+        ident = keep.tile([P, P], F32, name="ident", tag="ident")
+        make_identity(nc, ident[:])
+        bias = keep.tile([P, 2 * N], BF16, name="bias", tag="bias")
+        w2c = keep.tile([P, KP * 2 * N], U32, name="w2c", tag="w2c", align_bytes=64)
+        w2s = keep.tile([P, KP * 2 * N], U8, name="w2s", tag="w2s", align_bytes=64)
+        wvc = keep.tile([P, N], U32, name="wvc", tag="wvc", align_bytes=64)
+        wvs = keep.tile([P, N], U8, name="wvs", tag="wvs", align_bytes=64)
+        ssx = keep.tile([P, NT], F32, name="ssx", tag="ssx")
+        ssm = keep.tile([P, NT], F32, name="ssm", tag="ssm")
+        ssq = keep.tile([P, NT], F32, name="ssq", tag="ssq")
+        slv = keep.tile([P, NT], F32, name="slv", tag="slv")
+        bvx = keep.tile([P, NT], F32, name="bvx", tag="bvx")
+        lp = keep.tile([P, NT], F32, name="lp", tag="lp")
+
+        w2raw = {}
+        xraw = {}
+        hraw = {}
+        yraw = {}
+        eraw = {}
+        xc = {}
+        xs = {}
+        xg = {}
+        hg = {}
+        hc = {}
+        hs = {}
+        trb = {}
+        fmu = {}
+        flv = {}
+        mu = {}
+        lv = {}
+        std = {}
+        istd = {}
+        tt = {}
+        nd = {}
+        ee = {}
+        mt = {}
+        mg = {}
+        mc = {}
+        ms = {}
+        ub = {}
+        cc = {}
+        sm = {}
+
+        def load_w2(g):
+            w2raw[g] = work.tile([P, 4 * 2 * N], BF16, name="w2raw", tag="w2raw", bufs=3)
+            nc.sync.dma_start(
+                out=w2raw[g][:].rearrange("p (u z) -> p u z", u=2),
+                in_=W2[512 * g : 512 * (g + 1), :].rearrange("(u q e) c -> q u (e c)", u=2, e=2),
+            )
+
+        def load_wv():
+            w2raw["v"] = keep.tile([P, 4 * N], BF16, name="wvraw", tag="wvraw")
+            nc.sync.dma_start(
+                out=w2raw["v"][:].rearrange("p (u z) -> p u z", u=2),
+                in_=Wv.rearrange("(u q e) c -> q u (e c)", u=2, e=2),
+            )
+
+        def load_x(j):
+            xraw[j] = work.tile([P, 4 * N], BF16, name="xraw", tag="xraw", bufs=4)
+            nc.sync.dma_start(out=xraw[j][:].rearrange("p (i n) -> p i n", i=4), in_=x_v[:, 4 * j : 4 * j + 4, :])
+
+        def load_h(j):
+            hraw[j] = work.tile([P, 2 * H], BF16, name="hraw", tag="hraw", bufs=4)
+            nc.sync.dma_start(out=hraw[j][:].rearrange("p (i k) -> p i k", i=2), in_=h_v[:, 2 * j : 2 * j + 2, :])
+
+        def load_ye(j):
+            eraw[j] = work.tile([P, 4 * N], BF16, name="eraw", tag="eraw", bufs=3)
+            nc.sync.dma_start(out=eraw[j][:].rearrange("p (i n) -> p i n", i=4), in_=e_v[:, 4 * j : 4 * j + 4, :])
+            yraw[j] = work.tile([P, 4 * N], BF16, name="yraw", tag="yraw", bufs=3)
+            nc.sync.dma_start(out=yraw[j][:].rearrange("p (i n) -> p i n", i=4), in_=y_v[:, 4 * j : 4 * j + 4, :])
+
+        def regroup(eng_copy, raw, cols, width, name):
+            g_t = work.tile([P, 4 * width], BF16, name=name, tag="wgrp", bufs=4, align_bytes=64)
+            eng_copy(
+                out=g_t[:].rearrange("p (c i t) -> p c t i", i=4, t=4),
+                in_=raw[:].rearrange("p (t n) -> p t n", t=4)[:, :, cols].rearrange("p t (c i) -> p c t i", i=4),
+            )
+            return g_t
+
+        def quant(g_t, codes, scales):
+            nc.vector.quantize_mx(out=codes.bitcast(FP8X4), scales=scales, in_=g_t[:])
+
+        def x_transposes(j, pr):
+            t_ps = psum.tile([P, 4, P], F32, name="tr", tag="tr", bufs=2)
+            xw = xraw[j][:].bitcast(F32)
+            for q in range(4):
+                nc.tensor.transpose(t_ps[:, q, :], xw[:, 512 * pr + 128 * q : 512 * pr + 128 * (q + 1)], ident[:])
+            return t_ps
+
+        def x_copy(j, pr, t_ps):
+            if pr == 0:
+                xg[j] = work.tile([P, 4 * N], BF16, name="xg", tag="xg", bufs=2, align_bytes=64)
+            dst = xg[j][:].bitcast(F32).rearrange("p (i r u) -> p i r u", i=4, u=2)
+            nc.scalar.copy(out=dst[:, 2 * pr : 2 * pr + 2, :, :], in_=t_ps[:].rearrange("p (i u) r -> p i r u", u=2))
+
+        def x_quant(j):
+            xc[j] = keep.tile([P, N], U32, name="xc%d" % j, tag="xc%d" % j, align_bytes=64)
+            xs[j] = keep.tile([P, N], U8, name="xs%d" % j, tag="xs%d" % j, align_bytes=64)
+            quant(xg[j], xc[j][:], xs[j][:])
+
+        def x_matmul(i):
+            u_ps = psum.tile([P, N], F32, name="f", tag="f", bufs=4)
+            j = i // 4
+            r = i % 4
+            nc.tensor.matmul_mx(
+                out=u_ps[:],
+                lhsT=xc[j][:, P * r : P * (r + 1)].bitcast(FP8X4),
+                lhsT_scale=xs[j][:, P * r : P * (r + 1)],
+                rhs=wvc[:].bitcast(FP8X4),
+                rhs_scale=wvs[:],
+                start=True,
+                stop=True,
+            )
+            return u_ps
+
+        def square_sum(src, acc):
+            junk = work.tile([P, N], BF16, name="junk", tag="junk", bufs=2)
+            nc.scalar.activation(out=junk[:], in_=src, func=ACT.Square, accum_out=acc)
+
+        def x_bvx(j):
+            nc.vector.tensor_scalar(
+                out=bvx[:, 4 * j : 4 * j + 4], in0=ssx[:, 4 * j : 4 * j + 4], scalar1=1e-3, scalar2=0.99, op0=ALU.add, op1=ALU.mult
+            )
+
+        def ok(i):
+            return 0 <= i < NT
+
+        def TH(i):
+            hw = hraw[i // 2][:].bitcast(F32)
+            base = 1024 * (i % 2)
+            trb[i] = []
+            for b in range(2):
+                t_ps = psum.tile([P, 4, P], F32, name="tr", tag="tr", bufs=2)
+                for q in range(4):
+                    o = base + 512 * b + 128 * q
+                    nc.tensor.transpose(t_ps[:, q, :], hw[:, o : o + 128], ident[:])
+                trb[i].append(t_ps)
+
+        def CH(i, b):
+            if b == 0:
+                hg[i] = work.tile([P, H], BF16, name="hg", tag="hg", bufs=2, align_bytes=64)
+            dst = hg[i][:].bitcast(F32).rearrange("p (g r u) -> p g r u", g=4, u=2)
+            nc.scalar.copy(out=dst[:, 2 * b : 2 * b + 2, :, :], in_=trb[i][b][:].rearrange("p (g u) r -> p g r u", u=2))
+
+        def QH(i):
+            hc[i] = work.tile([P, N], U32, name="hc", tag="hc", bufs=3, align_bytes=64)
+            hs[i] = work.tile([P, N], U8, name="hs", tag="hs", bufs=3, align_bytes=64)
+            quant(hg[i], hc[i][:], hs[i][:])
+
+        def MF(i, half):
+            acc = psum.tile([P, N], F32, name="f", tag="f", bufs=4)
+            if half == 0:
+                fmu[i] = acc
+            else:
+                flv[i] = acc
+            if True:
+                for g in range(KP):
+                    o = 2 * N * g + N * half
+                    nc.tensor.matmul_mx(
+                        out=acc[:],
+                        lhsT=hc[i][:, P * g : P * (g + 1)].bitcast(FP8X4),
+                        lhsT_scale=hs[i][:, P * g : P * (g + 1)],
+                        rhs=w2c[:, o : o + N].bitcast(FP8X4),
+                        rhs_scale=w2s[:, o : o + N],
+                        start=(g == 0),
+                        stop=(g == KP - 1),
+                    )
+
+        def V1(i):
+            mu[i] = work.tile([P, N], F32, name="mu", tag="mu", bufs=4)
+            nc.vector.tensor_tensor(out=mu[i][:], in0=fmu[i][:], in1=bias[:, 0:N], op=ALU.add)
+
+        def V2(i):
+            lv[i] = work.tile([P, N], F32, name="lv", tag="lv", bufs=2)
+            nc.vector.scalar_tensor_tensor(
+                out=lv[i][:], in0=flv[i][:], scalar=1.0, in1=bias[:, N : 2 * N], op0=ALU.mult, op1=ALU.add, accum_out=slv[:, i : i + 1]
+            )
+
+        def TM(i):
+            mt[i] = psum.tile([P, 4, P], F32, name="mt", tag="mt", bufs=1)
+            src = mu[i][:].rearrange("p (u q e) -> p u e q", u=2, e=2)
+            for t in range(4):
+                nc.tensor.transpose(mt[i][:, t, :], src[:, t // 2, t % 2, :], ident[:])
+
+        def CM(i):
+            mg[i] = work.tile([P, N], BF16, name="mg", tag="mg", bufs=2, align_bytes=64)
+            nc.scalar.copy(out=mg[i][:].rearrange("p (r t) -> p r t", t=4), in_=mt[i][:].rearrange("p t r -> p r t"))
+
+        def QM(i):
+            mc[i] = work.tile([P, P], U32, name="mc", tag="mc", bufs=2, align_bytes=64)
+            ms[i] = work.tile([P, P], U8, name="ms", tag="ms", bufs=2, align_bytes=64)
+            quant(mg[i], mc[i][:], ms[i][:])
+
+        def MU(i):
+            ub[i] = psum.tile([P, N], F32, name="u", tag="u", bufs=1)
+            nc.tensor.matmul_mx(
+                out=ub[i][:],
+                lhsT=mc[i][:].bitcast(FP8X4),
+                lhsT_scale=ms[i][:],
+                rhs=wvc[:].bitcast(FP8X4),
+                rhs_scale=wvs[:],
+                start=True,
+                stop=True,
+            )
+
+        def SU(i):
+            square_sum(ub[i][:], ssm[:, i : i + 1])
+
+        def SE(i):
+            std[i] = work.tile([P, N], F32, name="std", tag="std", bufs=2)
+            nc.scalar.activation(out=std[i][:], in_=lv[i][:], func=ACT.Exp, scale=0.5)
+            istd[i] = work.tile([P, N], F32, name="istd", tag="istd", bufs=4)
+            nc.scalar.activation(out=istd[i][:], in_=lv[i][:], func=ACT.Exp, scale=-0.5)
+
+        def VT(i):
+            tt[i] = work.tile([P, N], F32, name="tt", tag="tt", bufs=3)
+            eng = nc.gpsimd if T_ON_GPSIMD else nc.vector
+            eng.tensor_tensor(out=tt[i][:], in0=std[i][:], in1=eraw[i // 4][:, N * (i % 4) : N * (i % 4 + 1)], op=ALU.mult)
+
+        def T1(i):
+            sm[i] = work.tile([P, 4], F32, name="sm", tag="sm", bufs=4)
+            nc.vector.tensor_scalar(
+                out=sm[i][:, 0:1], in0=ssm[:, i : i + 1], scalar1=1e-3, scalar2=bvx[:, i : i + 1], op0=ALU.add, op1=ALU.max
+            )
+
+        def T2(i):
+            nc.vector.reciprocal(out=sm[i][:, 1:2], in_=sm[i][:, 0:1])
+
+        def T3(i):
+            nc.vector.tensor_scalar(out=sm[i][:, 2:3], in0=sm[i][:, 1:2], scalar1=bvx[:, i : i + 1], scalar2=None, op0=ALU.mult)
+
+        def ND(i):
+            nd[i] = work.tile([P, N], F32, name="nd", tag="nd", bufs=2)
+            nc.vector.scalar_tensor_tensor(
+                out=nd[i][:], in0=mu[i][:], scalar=sm[i][:, 2:3], in1=yraw[i // 4][:, N * (i % 4) : N * (i % 4 + 1)], op0=ALU.mult, op1=ALU.subtract
+            )
+
+        def FX(i):
+            fx = work.tile([P, N], F32, name="fx", tag="fx", bufs=3)
+            nc.vector.scalar_tensor_tensor(out=fx[:], in0=mu[i][:], scalar=sm[i][:, 2:3], in1=tt[i][:], op0=ALU.mult, op1=ALU.add)
+            nc.sync.dma_start(out=fx_v[:, i, :], in_=fx[:])
+
+        def EE(i):
+            ee[i] = work.tile([P, N], F32, name="ee", tag="ee", bufs=2)
+            nc.vector.tensor_tensor(out=ee[i][:], in0=nd[i][:], in1=istd[i][:], op=ALU.mult)
+
+        def SQ(i):
+            square_sum(ee[i][:], ssq[:, i : i + 1])
+
+        def x_front(j):
+            for pr in range(2):
+                x_copy(j, pr, x_transposes(j, pr))
+
+        def x_mm(j):
+            return [x_matmul(i) for i in range(4 * j, 4 * j + 4)]
+
+        def x_sq(j, banks):
+            for r in range(4):
+                square_sum(banks[r][:], ssx[:, 4 * j + r : 4 * j + r + 1])
+
+        def w2_rg(g, half, eng_copy):
+            wg[(g, half)] = regroup(eng_copy, w2raw[g], slice(N * half, N * (half + 1)), N, "w2g")
+
+        def w2_q(g, half):
+            o = 2 * N * g + N * half
+            quant(wg[(g, half)], w2c[:, o : o + N], w2s[:, o : o + N])
+
+        wg = {}
+        vcopy = nc.vector.tensor_copy
+        load_wv()
+        load_w2(0)
+        load_x(0)
+        load_w2(1)
+        load_x(1)
+        load_w2(2)
+        load_x(2)
+        load_h(0)
+
+        wvg = regroup(vcopy, w2raw["v"], slice(0, N), N, "wvg")
+        quant(wvg, wvc[:], wvs[:])
+        x_front(0)
+        w2_rg(0, 0, vcopy)
+        w2_rg(0, 1, vcopy)
+        load_w2(3)
+        load_h(1)
+        nc.sync.dma_start(out=bias[:], in_=b2.partition_broadcast(P))
+        load_ye(0)
+        load_x(3)
+        load_h(2)
+        load_h(3)
+        load_ye(1)
+        w2_q(0, 0)
+        w2_q(0, 1)
+        x_quant(0)
+        x_front(1)
+        ux = x_mm(0)
+        x_sq(0, ux)
+        w2_rg(1, 0, vcopy)
+        w2_rg(1, 1, vcopy)
+        w2_q(1, 0)
+        w2_q(1, 1)
+        x_quant(1)
+        x_front(2)
+        ux = x_mm(1)
+        TH(0)
+        CH(0, 0)
+        CH(0, 1)
+        x_sq(1, ux)
+        w2_rg(2, 0, vcopy)
+        x_quant(2)
+        w2_q(2, 0)
+        QH(0)
+        TH(1)
+        CH(1, 0)
+        CH(1, 1)
+        w2_rg(3, 0, vcopy)
+        w2_rg(2, 1, vcopy)
+        w2_q(3, 0)
+        MF(0, 0)
+        QH(1)
+        w2_rg(3, 1, vcopy)
+        w2_q(2, 1)
+        TH(2)
+        CH(2, 0)
+        CH(2, 1)
+        V1(0)
+        TM(0)
+        w2_q(3, 1)
+        MF(1, 0)
+        MF(0, 1)
+        CM(0)
+        QH(2)
+        x_bvx(0)
+        x_bvx(1)
+        QM(0)
+        MU(0)
+        TH(3)
+        CH(3, 0)
+        CH(3, 1)
+
+        for a in range(0, NT + 2):
+            xk = a + 8 if a + 8 < NT else -1
+            if a >= 1 and a % 2 == 1 and (a + 7) // 2 < NT // 2:
+                load_h((a + 7) // 2)
+            if a == 2:
+                load_ye(2)
+            if a == 6:
+                load_ye(3)
+            if ok(a + 4):
+                TH(a + 4)
+            if ok(a + 1):
+                V1(a + 1)
+                TM(a + 1)
+            if ok(a):
+                V2(a)
+                SU(a)
+                T1(a)
+            if ok(a + 4):
+                CH(a + 4, 0)
+            if ok(a + 3):
+                QH(a + 3)
+            if a == 1:
+                x_front(3)
+            if a == 2:
+                x_quant(3)
+            if ok(a):
+                T2(a)
+            if ok(a + 1):
+                CM(a + 1)
+            if ok(a - 1):
+                EE(a - 1)
+            if xk >= 0:
+                ub["x"] = psum.tile([P, N], F32, name="u", tag="u", bufs=1)
+                nc.tensor.matmul_mx(
+                    out=ub["x"][:],
+                    lhsT=xc[xk // 4][:, P * (xk % 4) : P * (xk % 4 + 1)].bitcast(FP8X4),
+                    lhsT_scale=xs[xk // 4][:, P * (xk % 4) : P * (xk % 4 + 1)],
+                    rhs=wvc[:].bitcast(FP8X4),
+                    rhs_scale=wvs[:],
+                    start=True,
+                    stop=True,
+                )
+                square_sum(ub["x"][:], ssx[:, xk : xk + 1])
+            if a == 4:
+                x_bvx(2)
+            if a == 8:
+                x_bvx(3)
+            if ok(a + 1):
+                MF(a + 1, 1)
+            if ok(a + 2):
+                MF(a + 2, 0)
+            if ok(a):
+                SE(a)
+                T3(a)
+                ND(a)
+            if ok(a + 1):
+                QM(a + 1)
+                MU(a + 1)
+            if T_ON_GPSIMD:
+                if ok(a):
+                    VT(a)
+                if ok(a - 1):
+                    FX(a - 1)
+            elif ok(a):
+                VT(a)
+                FX(a)
+            if ok(a - 1):
+                SQ(a - 1)
+            if ok(a + 4):
+                CH(a + 4, 1)
+
+        nc.vector.tensor_tensor(out=lp[:], in0=slv[:], in1=ssq[:], op=ALU.add)
+        nc.vector.tensor_scalar(
+            out=lp[:], in0=lp[:], scalar1=-0.5, scalar2=-0.5 * N * math.log(2.0 * math.pi), op0=ALU.mult, op1=ALU.add
+        )
+        nc.sync.dma_start(out=lp_v, in_=lp[:])

@@ -140,7 +140,7 @@ def tile_mdn_module_pa_kernel(tc, h, W2, b2, x, y, eps, Wv, out_0, out_1):
             quant(xg[j], xc[j][:], xs[j][:])
 
         def x_matmul(i):
-            u_ps = psum.tile([P, N], F32, name="f", tag="f", bufs=4)
+            u_ps = psum.tile([P, N], F32, name="f", tag="f", bufs=3)
             j = i // 4
             r = i % 4
             nc.tensor.matmul_mx(
@@ -184,12 +184,12 @@ def tile_mdn_module_pa_kernel(tc, h, W2, b2, x, y, eps, Wv, out_0, out_1):
             nc.scalar.copy(out=dst[:, 2 * b : 2 * b + 2, :, :], in_=trb[i][b][:].rearrange("p (g u) r -> p g r u", u=2))
 
         def QH(i):
-            hc[i] = work.tile([P, N], U32, name="hc", tag="hc", bufs=3, align_bytes=64)
-            hs[i] = work.tile([P, N], U8, name="hs", tag="hs", bufs=3, align_bytes=64)
+            hc[i] = work.tile([P, N], U32, name="hc", tag="hc", bufs=4, align_bytes=64)
+            hs[i] = work.tile([P, N], U8, name="hs", tag="hs", bufs=4, align_bytes=64)
             quant(hg[i], hc[i][:], hs[i][:])
 
         def MF(i, half):
-            acc = psum.tile([P, N], F32, name="f", tag="f", bufs=4)
+            acc = psum.tile([P, N], F32, name="f", tag="f", bufs=3)
             if half == 0:
                 fmu[i] = acc
             else:
@@ -212,7 +212,7 @@ def tile_mdn_module_pa_kernel(tc, h, W2, b2, x, y, eps, Wv, out_0, out_1):
             nc.vector.tensor_tensor(out=mu[i][:], in0=fmu[i][:], in1=bias[:, 0:N], op=ALU.add)
 
         def V2(i):
-            lv[i] = work.tile([P, N], F32, name="lv", tag="lv", bufs=2)
+            lv[i] = work.tile([P, N], F32, name="lv", tag="lv", bufs=3)
             nc.vector.scalar_tensor_tensor(
                 out=lv[i][:], in0=flv[i][:], scalar=1.0, in1=bias[:, N : 2 * N], op0=ALU.mult, op1=ALU.add, accum_out=slv[:, i : i + 1]
             )
@@ -247,14 +247,31 @@ def tile_mdn_module_pa_kernel(tc, h, W2, b2, x, y, eps, Wv, out_0, out_1):
         def SU(i):
             square_sum(ub[i][:], ssm[:, i : i + 1])
 
-        def SE(i):
+        def SD(i):
             std[i] = work.tile([P, N], F32, name="std", tag="std", bufs=2)
             nc.scalar.activation(out=std[i][:], in_=lv[i][:], func=ACT.Exp, scale=0.5)
-            istd[i] = work.tile([P, N], F32, name="istd", tag="istd", bufs=4)
+
+        def SI(i):
+            istd[i] = work.tile([P, N], F32, name="istd", tag="istd", bufs=3)
             nc.scalar.activation(out=istd[i][:], in_=lv[i][:], func=ACT.Exp, scale=-0.5)
 
+        def UX(k):
+            ub["x"] = psum.tile([P, N], F32, name="ux", tag="ux", bufs=1)
+            nc.tensor.matmul_mx(
+                out=ub["x"][:],
+                lhsT=xc[k // 4][:, P * (k % 4) : P * (k % 4 + 1)].bitcast(FP8X4),
+                lhsT_scale=xs[k // 4][:, P * (k % 4) : P * (k % 4 + 1)],
+                rhs=wvc[:].bitcast(FP8X4),
+                rhs_scale=wvs[:],
+                start=True,
+                stop=True,
+            )
+
+        def SX(k):
+            square_sum(ub["x"][:], ssx[:, k : k + 1])
+
         def VT(i):
-            tt[i] = work.tile([P, N], F32, name="tt", tag="tt", bufs=3)
+            tt[i] = work.tile([P, N], F32, name="tt", tag="tt", bufs=2)
             eng = nc.gpsimd if T_ON_GPSIMD else nc.vector
             eng.tensor_tensor(out=tt[i][:], in0=std[i][:], in1=eraw[i // 4][:, N * (i % 4) : N * (i % 4 + 1)], op=ALU.mult)
 
@@ -292,12 +309,9 @@ def tile_mdn_module_pa_kernel(tc, h, W2, b2, x, y, eps, Wv, out_0, out_1):
             for pr in range(2):
                 x_copy(j, pr, x_transposes(j, pr))
 
-        def x_mm(j):
-            return [x_matmul(i) for i in range(4 * j, 4 * j + 4)]
-
-        def x_sq(j, banks):
-            for r in range(4):
-                square_sum(banks[r][:], ssx[:, 4 * j + r : 4 * j + r + 1])
+        def x_back(j):
+            for i in range(4 * j, 4 * j + 4):
+                square_sum(x_matmul(i)[:], ssx[:, i : i + 1])
 
         def w2_rg(g, half, eng_copy):
             wg[(g, half)] = regroup(eng_copy, w2raw[g], slice(N * half, N * (half + 1)), N, "w2g")
@@ -308,13 +322,17 @@ def tile_mdn_module_pa_kernel(tc, h, W2, b2, x, y, eps, Wv, out_0, out_1):
 
         wg = {}
         vcopy = nc.vector.tensor_copy
+        brow = keep.tile([P, 2 * N], BF16, name="brow", tag="brow")
+        ones = keep.tile([P, P], BF16, name="ones", tag="ones")
+        nc.vector.memset(brow[:], 0.0)
+        nc.vector.memset(ones[:], 1.0)
+        nc.scalar.dma_start(out=brow[0:1, :], in_=b2.rearrange("(o n) -> o n", o=1))
         load_wv()
         load_w2(0)
         load_x(0)
         load_w2(1)
         load_x(1)
         load_w2(2)
-        load_x(2)
         load_h(0)
 
         wvg = regroup(vcopy, w2raw["v"], slice(0, N), N, "wvg")
@@ -324,131 +342,105 @@ def tile_mdn_module_pa_kernel(tc, h, W2, b2, x, y, eps, Wv, out_0, out_1):
         w2_rg(0, 1, vcopy)
         load_w2(3)
         load_h(1)
-        nc.sync.dma_start(out=bias[:], in_=b2.partition_broadcast(P))
+        load_x(2)
         load_ye(0)
-        load_x(3)
         load_h(2)
+        load_x(3)
         load_h(3)
         load_ye(1)
         w2_q(0, 0)
         w2_q(0, 1)
         x_quant(0)
         x_front(1)
-        ux = x_mm(0)
-        x_sq(0, ux)
+        x_back(0)
         w2_rg(1, 0, vcopy)
         w2_rg(1, 1, vcopy)
         w2_q(1, 0)
         w2_q(1, 1)
         x_quant(1)
-        x_front(2)
-        ux = x_mm(1)
-        TH(0)
-        CH(0, 0)
-        CH(0, 1)
-        x_sq(1, ux)
+        x_back(1)
+        for half in range(2):
+            b_ps = psum.tile([P, N], F32, name="f", tag="f", bufs=3)
+            nc.tensor.matmul(out=b_ps[:], lhsT=ones[:], rhs=brow[:, N * half : N * (half + 1)], start=True, stop=True)
+            nc.scalar.copy(out=bias[:, N * half : N * (half + 1)], in_=b_ps[:])
         w2_rg(2, 0, vcopy)
-        x_quant(2)
-        w2_q(2, 0)
-        QH(0)
-        TH(1)
-        CH(1, 0)
-        CH(1, 1)
-        w2_rg(3, 0, vcopy)
         w2_rg(2, 1, vcopy)
-        w2_q(3, 0)
-        MF(0, 0)
-        QH(1)
-        w2_rg(3, 1, vcopy)
-        w2_q(2, 1)
-        TH(2)
-        CH(2, 0)
-        CH(2, 1)
-        V1(0)
-        TM(0)
-        w2_q(3, 1)
-        MF(1, 0)
-        MF(0, 1)
-        CM(0)
-        QH(2)
+        w2_q(2, 0)
         x_bvx(0)
         x_bvx(1)
-        QM(0)
-        MU(0)
-        TH(3)
-        CH(3, 0)
-        CH(3, 1)
 
-        for a in range(0, NT + 2):
-            xk = a + 8 if a + 8 < NT else -1
+        for a in range(-4, NT + 3):
+            xk = a + 9
             if a >= 1 and a % 2 == 1 and (a + 7) // 2 < NT // 2:
                 load_h((a + 7) // 2)
             if a == 2:
                 load_ye(2)
             if a == 6:
                 load_ye(3)
+            if ok(a - 1):
+                SI(a - 1)
+            if 8 <= xk - 1 < NT:
+                SX(xk - 1)
+            if a == -2:
+                x_front(2)
+            if a == 1:
+                x_front(3)
             if ok(a + 4):
                 TH(a + 4)
             if ok(a + 1):
                 V1(a + 1)
-                TM(a + 1)
+            if ok(a):
+                QM(a)
+            if ok(a - 1):
+                T1(a - 1)
             if ok(a):
                 V2(a)
-                SU(a)
-                T1(a)
-            if ok(a + 4):
-                CH(a + 4, 0)
+            if ok(a - 1):
+                T2(a - 1)
             if ok(a + 3):
                 QH(a + 3)
-            if a == 1:
-                x_front(3)
+            if a == -3:
+                w2_rg(3, 0, vcopy)
+                w2_q(2, 1)
+                w2_q(3, 0)
+            if a == -2:
+                w2_rg(3, 1, vcopy)
+            if a == -1:
+                w2_q(3, 1)
+                x_quant(2)
             if a == 2:
                 x_quant(3)
-            if ok(a):
-                T2(a)
-            if ok(a + 1):
-                CM(a + 1)
-            if ok(a - 1):
-                EE(a - 1)
-            if xk >= 0:
-                ub["x"] = psum.tile([P, N], F32, name="u", tag="u", bufs=1)
-                nc.tensor.matmul_mx(
-                    out=ub["x"][:],
-                    lhsT=xc[xk // 4][:, P * (xk % 4) : P * (xk % 4 + 1)].bitcast(FP8X4),
-                    lhsT_scale=xs[xk // 4][:, P * (xk % 4) : P * (xk % 4 + 1)],
-                    rhs=wvc[:].bitcast(FP8X4),
-                    rhs_scale=wvs[:],
-                    start=True,
-                    stop=True,
-                )
-                square_sum(ub["x"][:], ssx[:, xk : xk + 1])
             if a == 4:
                 x_bvx(2)
             if a == 8:
                 x_bvx(3)
-            if ok(a + 1):
-                MF(a + 1, 1)
+            if ok(a - 1):
+                T3(a - 1)
+                VT(a - 1)
+            if ok(a - 2):
+                EE(a - 2)
+            if ok(a - 1):
+                ND(a - 1)
+                FX(a - 1)
             if ok(a + 2):
                 MF(a + 2, 0)
             if ok(a):
-                SE(a)
-                T3(a)
-                ND(a)
+                MU(a)
             if ok(a + 1):
-                QM(a + 1)
-                MU(a + 1)
-            if T_ON_GPSIMD:
-                if ok(a):
-                    VT(a)
-                if ok(a - 1):
-                    FX(a - 1)
-            elif ok(a):
-                VT(a)
-                FX(a)
-            if ok(a - 1):
-                SQ(a - 1)
+                TM(a + 1)
+                MF(a + 1, 1)
+            if 8 <= xk < NT:
+                UX(xk)
             if ok(a + 4):
+                CH(a + 4, 0)
                 CH(a + 4, 1)
+            if ok(a):
+                SD(a)
+                SU(a)
+            if ok(a + 1):
+                CM(a + 1)
+            if ok(a - 2):
+                SQ(a - 2)
 
         nc.vector.tensor_tensor(out=lp[:], in0=slv[:], in1=ssq[:], op=ALU.add)
         nc.vector.tensor_scalar(

@@ -20,7 +20,7 @@ NT = B // P
 KP = H // 512
 FLOPS = 2 * B * H * 2 * N + 2 * 2 * B * N * N
 
-T_ON_GPSIMD = False
+T_ON_GPSIMD = True
 S_HALVES = ()
 
 
@@ -121,8 +121,8 @@ def tile_mdn_module_pa_kernel(tc, h, W2, b2, x, y, eps, Wv, out_0, out_1):
         def quant(g_t, codes, scales):
             nc.vector.quantize_mx(out=codes.bitcast(FP8X4), scales=scales, in_=g_t[:])
 
-        def x_transposes(j, pr):
-            t_ps = psum.tile([P, 4, P], F32, name="tr", tag="tr", bufs=2)
+        def x_transposes(j, pr, tag="tr", bufs=2):
+            t_ps = psum.tile([P, 4, P], F32, name=tag, tag=tag, bufs=bufs)
             xw = xraw[j][:].bitcast(F32)
             for q in range(4):
                 nc.tensor.transpose(t_ps[:, q, :], xw[:, 512 * pr + 128 * q : 512 * pr + 128 * (q + 1)], ident[:])
@@ -358,6 +358,9 @@ def tile_mdn_module_pa_kernel(tc, h, W2, b2, x, y, eps, Wv, out_0, out_1):
         w2_q(1, 0)
         w2_q(1, 1)
         x_quant(1)
+        TH(0)
+        CH(0, 0)
+        CH(0, 1)
         x_back(1)
         for half in range(2):
             b_ps = psum.tile([P, N], F32, name="f", tag="f", bufs=3)
@@ -366,11 +369,12 @@ def tile_mdn_module_pa_kernel(tc, h, W2, b2, x, y, eps, Wv, out_0, out_1):
         w2_rg(2, 0, vcopy)
         w2_rg(2, 1, vcopy)
         w2_q(2, 0)
-        x_bvx(0)
-        x_bvx(1)
+        TH(1)
 
-        for a in range(-4, NT + 3):
-            xk = a + 9
+        xt = {}
+        for a in range(-3, NT + 3):
+            xk = a + 6
+            xp = a + 1
             if a >= 1 and a % 2 == 1 and (a + 7) // 2 < NT // 2:
                 load_h((a + 7) // 2)
             if a == 2:
@@ -381,44 +385,57 @@ def tile_mdn_module_pa_kernel(tc, h, W2, b2, x, y, eps, Wv, out_0, out_1):
                 SI(a - 1)
             if 8 <= xk - 1 < NT:
                 SX(xk - 1)
-            if a == -2:
-                x_front(2)
-            if a == 1:
-                x_front(3)
+            if 0 <= xp - 1 < 4:
+                x_copy(2 + (xp - 1) // 2, (xp - 1) % 2, xt[xp - 1])
             if ok(a + 4):
-                TH(a + 4)
+                CH(a + 4, 0)
+                CH(a + 4, 1)
             if ok(a + 1):
                 V1(a + 1)
+            if T_ON_GPSIMD and ok(a):
+                V2(a)
             if ok(a):
                 QM(a)
             if ok(a - 1):
                 T1(a - 1)
-            if ok(a):
+            if ok(a) and not T_ON_GPSIMD:
                 V2(a)
-            if ok(a - 1):
-                T2(a - 1)
-            if ok(a + 3):
-                QH(a + 3)
             if a == -3:
                 w2_rg(3, 0, vcopy)
                 w2_q(2, 1)
+            if T_ON_GPSIMD and ok(a + 3):
+                QH(a + 3)
+            if ok(a - 1):
+                T2(a - 1)
+            if ok(a + 3) and not T_ON_GPSIMD:
+                QH(a + 3)
+            if a == -3:
                 w2_q(3, 0)
             if a == -2:
                 w2_rg(3, 1, vcopy)
+                x_bvx(0)
+                x_bvx(1)
             if a == -1:
                 w2_q(3, 1)
+            if a == 1:
                 x_quant(2)
-            if a == 2:
+            if a == 3:
                 x_quant(3)
-            if a == 4:
+            if a == 7:
                 x_bvx(2)
-            if a == 8:
+            if a == 11:
                 x_bvx(3)
-            if ok(a - 1):
-                T3(a - 1)
-                VT(a - 1)
-            if ok(a - 2):
-                EE(a - 2)
+            if T_ON_GPSIMD:
+                if ok(a - 2):
+                    EE(a - 2)
+                if ok(a - 1):
+                    T3(a - 1)
+            else:
+                if ok(a - 1):
+                    T3(a - 1)
+                    VT(a - 1)
+                if ok(a - 2):
+                    EE(a - 2)
             if ok(a - 1):
                 ND(a - 1)
                 FX(a - 1)
@@ -431,16 +448,19 @@ def tile_mdn_module_pa_kernel(tc, h, W2, b2, x, y, eps, Wv, out_0, out_1):
                 MF(a + 1, 1)
             if 8 <= xk < NT:
                 UX(xk)
-            if ok(a + 4):
-                CH(a + 4, 0)
-                CH(a + 4, 1)
             if ok(a):
                 SD(a)
+                if T_ON_GPSIMD:
+                    VT(a)
                 SU(a)
             if ok(a + 1):
                 CM(a + 1)
             if ok(a - 2):
                 SQ(a - 2)
+            if 0 <= xp < 4:
+                xt[xp] = x_transposes(2 + xp // 2, xp % 2, "mt", 1)
+            if ok(a + 5):
+                TH(a + 5)
 
         nc.vector.tensor_tensor(out=lp[:], in0=slv[:], in1=ssq[:], op=ALU.add)
         nc.vector.tensor_scalar(

@@ -46,6 +46,8 @@ def tile_mdn_module_pa_kernel(tc, h, W2, b2, x, y, eps, Wv, out_0, out_1):
         w2s = keep.tile([P, KP * 2 * N], U8, name="w2s", tag="w2s", align_bytes=64)
         wvc = keep.tile([P, N], U32, name="wvc", tag="wvc", align_bytes=64)
         wvs = keep.tile([P, N], U8, name="wvs", tag="wvs", align_bytes=64)
+        wmc = keep.tile([P, N], U32, name="wmc", tag="wmc", align_bytes=64)
+        wms = keep.tile([P, N], U8, name="wms", tag="wms", align_bytes=64)
         ssx = keep.tile([P, NT], F32, name="ssx", tag="ssx")
         ssm = keep.tile([P, NT], F32, name="ssm", tag="ssm")
         ssq = keep.tile([P, NT], F32, name="ssq", tag="ssq")
@@ -95,6 +97,10 @@ def tile_mdn_module_pa_kernel(tc, h, W2, b2, x, y, eps, Wv, out_0, out_1):
                 out=w2raw["v"][:].rearrange("p (u z) -> p u z", u=2),
                 in_=Wv.rearrange("(u q e) c -> q u (e c)", u=2, e=2),
             )
+
+        def load_wm():
+            w2raw["m"] = keep.tile([P, 4 * N], BF16, name="wmraw", tag="wmraw")
+            nc.sync.dma_start(out=w2raw["m"][:].rearrange("p (t c) -> p t c", t=4), in_=Wv.rearrange("(t p) c -> p t c", t=4))
 
         def load_x(j):
             xraw[j] = work.tile([P, 4 * N], BF16, name="xraw", tag="xraw", bufs=4)
@@ -219,9 +225,8 @@ def tile_mdn_module_pa_kernel(tc, h, W2, b2, x, y, eps, Wv, out_0, out_1):
 
         def TM(i):
             mt[i] = psum.tile([P, 4, P], F32, name="mt", tag="mt", bufs=1)
-            src = mu[i][:].rearrange("p (u q e) -> p u e q", u=2, e=2)
             for t in range(4):
-                nc.tensor.transpose(mt[i][:, t, :], src[:, t // 2, t % 2, :], ident[:])
+                nc.tensor.transpose(mt[i][:, t, :], mu[i][:, P * t : P * (t + 1)], ident[:])
 
         def CM(i):
             mg[i] = work.tile([P, N], BF16, name="mg", tag="mg", bufs=2, align_bytes=64)
@@ -238,8 +243,8 @@ def tile_mdn_module_pa_kernel(tc, h, W2, b2, x, y, eps, Wv, out_0, out_1):
                 out=ub[i][:],
                 lhsT=mc[i][:].bitcast(FP8X4),
                 lhsT_scale=ms[i][:],
-                rhs=wvc[:].bitcast(FP8X4),
-                rhs_scale=wvs[:],
+                rhs=wmc[:].bitcast(FP8X4),
+                rhs_scale=wms[:],
                 start=True,
                 stop=True,
             )
@@ -328,53 +333,56 @@ def tile_mdn_module_pa_kernel(tc, h, W2, b2, x, y, eps, Wv, out_0, out_1):
         nc.vector.memset(ones[:], 1.0)
         nc.scalar.dma_start(out=brow[0:1, :], in_=b2.rearrange("(o n) -> o n", o=1))
         load_wv()
-        load_w2(0)
         load_x(0)
-        load_w2(1)
         load_x(1)
+        load_w2(0)
+        load_w2(1)
+        load_x(2)
         load_w2(2)
+        load_x(3)
         load_h(0)
 
         wvg = regroup(vcopy, w2raw["v"], slice(0, N), N, "wvg")
         quant(wvg, wvc[:], wvs[:])
         x_front(0)
+        x_quant(0)
+        x_front(1)
+        x_quant(1)
+        x_back(0)
         w2_rg(0, 0, vcopy)
         w2_rg(0, 1, vcopy)
         load_w2(3)
         load_h(1)
-        load_x(2)
+        load_wm()
         load_ye(0)
         load_h(2)
-        load_x(3)
         load_h(3)
         load_ye(1)
         w2_q(0, 0)
         w2_q(0, 1)
-        x_quant(0)
-        x_front(1)
-        x_back(0)
+        x_back(1)
+        x_front(2)
         w2_rg(1, 0, vcopy)
         w2_rg(1, 1, vcopy)
         w2_q(1, 0)
         w2_q(1, 1)
-        x_quant(1)
-        TH(0)
-        CH(0, 0)
-        CH(0, 1)
-        x_back(1)
+        x_front(3)
+        w2_rg(2, 0, vcopy)
+        w2_rg(2, 1, vcopy)
+        w2_q(2, 0)
+        w2_q(2, 1)
         for half in range(2):
             b_ps = psum.tile([P, N], F32, name="f", tag="f", bufs=3)
             nc.tensor.matmul(out=b_ps[:], lhsT=ones[:], rhs=brow[:, N * half : N * (half + 1)], start=True, stop=True)
             nc.scalar.copy(out=bias[:, N * half : N * (half + 1)], in_=b_ps[:])
-        w2_rg(2, 0, vcopy)
-        w2_rg(2, 1, vcopy)
-        w2_q(2, 0)
+        TH(0)
+        CH(0, 0)
+        CH(0, 1)
         TH(1)
 
         xt = {}
         for a in range(-3, NT + 3):
-            xk = a + 6
-            xp = a + 1
+            xk = 10 + 2 * a
             if a >= 1 and a % 2 == 1 and (a + 7) // 2 < NT // 2:
                 load_h((a + 7) // 2)
             if a == 2:
@@ -385,11 +393,11 @@ def tile_mdn_module_pa_kernel(tc, h, W2, b2, x, y, eps, Wv, out_0, out_1):
                 SI(a - 1)
             if 8 <= xk - 1 < NT:
                 SX(xk - 1)
-            if 0 <= xp - 1 < 4:
-                x_copy(2 + (xp - 1) // 2, (xp - 1) % 2, xt[xp - 1])
             if ok(a + 4):
                 CH(a + 4, 0)
                 CH(a + 4, 1)
+            if a == -2:
+                wg["m"] = regroup(nc.scalar.copy, w2raw["m"], slice(0, N), N, "wmg")
             if ok(a + 1):
                 V1(a + 1)
             if T_ON_GPSIMD and ok(a):
@@ -402,7 +410,6 @@ def tile_mdn_module_pa_kernel(tc, h, W2, b2, x, y, eps, Wv, out_0, out_1):
                 V2(a)
             if a == -3:
                 w2_rg(3, 0, vcopy)
-                w2_q(2, 1)
             if T_ON_GPSIMD and ok(a + 3):
                 QH(a + 3)
             if ok(a - 1):
@@ -413,17 +420,16 @@ def tile_mdn_module_pa_kernel(tc, h, W2, b2, x, y, eps, Wv, out_0, out_1):
                 w2_q(3, 0)
             if a == -2:
                 w2_rg(3, 1, vcopy)
+                x_quant(2)
                 x_bvx(0)
                 x_bvx(1)
             if a == -1:
                 w2_q(3, 1)
-            if a == 1:
-                x_quant(2)
-            if a == 3:
+                quant(wg["m"], wmc[:], wms[:])
                 x_quant(3)
-            if a == 7:
+            if a == 2:
                 x_bvx(2)
-            if a == 11:
+            if a == 4:
                 x_bvx(3)
             if T_ON_GPSIMD:
                 if ok(a - 2):
@@ -441,24 +447,29 @@ def tile_mdn_module_pa_kernel(tc, h, W2, b2, x, y, eps, Wv, out_0, out_1):
                 FX(a - 1)
             if ok(a + 2):
                 MF(a + 2, 0)
+            elif ok(a + 1):
+                TM(a + 1)
             if ok(a):
                 MU(a)
-            if ok(a + 1):
-                TM(a + 1)
-                MF(a + 1, 1)
             if 8 <= xk < NT:
                 UX(xk)
+            if ok(a + 2) and ok(a + 1):
+                TM(a + 1)
+            if ok(a + 1):
+                MF(a + 1, 1)
             if ok(a):
                 SD(a)
                 if T_ON_GPSIMD:
                     VT(a)
+            if 8 <= xk < NT:
+                SX(xk)
+                UX(xk + 1)
+            if ok(a):
                 SU(a)
             if ok(a + 1):
                 CM(a + 1)
             if ok(a - 2):
                 SQ(a - 2)
-            if 0 <= xp < 4:
-                xt[xp] = x_transposes(2 + xp // 2, xp % 2, "mt", 1)
             if ok(a + 5):
                 TH(a + 5)
 

@@ -276,7 +276,7 @@ def tile_mdn_module_pa_kernel(tc, h, W2, b2, x, y, eps, Wv, out_0, out_1):
             square_sum(ub["x"][:], ssx[:, k : k + 1])
 
         def VT(i):
-            tt[i] = work.tile([P, N], F32, name="tt", tag="tt", bufs=2)
+            tt[i] = work.tile([P, N], F32, name="tt", tag="tt", bufs=1)
             eng = nc.gpsimd if T_ON_GPSIMD else nc.vector
             eng.tensor_tensor(out=tt[i][:], in0=std[i][:], in1=eraw[i // 4][:, N * (i % 4) : N * (i % 4 + 1)], op=ALU.mult)
 

@@ -22,6 +22,7 @@ FLOPS = 2 * B * H * 2 * N + 2 * 2 * B * N * N
 
 T_ON_GPSIMD = True
 S_HALVES = ()
+V_CM = 0
 
 
 def tile_mdn_module_pa_kernel(tc, h, W2, b2, x, y, eps, Wv, out_0, out_1):
@@ -224,13 +225,14 @@ def tile_mdn_module_pa_kernel(tc, h, W2, b2, x, y, eps, Wv, out_0, out_1):
             )
 
         def TM(i):
-            mt[i] = psum.tile([P, 4, P], F32, name="mt", tag="mt", bufs=1)
+            mt[i] = psum.tile([P, 4, P], F32, name="mt", tag="mt", bufs=2)
             for t in range(4):
                 nc.tensor.transpose(mt[i][:, t, :], mu[i][:, P * t : P * (t + 1)], ident[:])
 
         def CM(i):
             mg[i] = work.tile([P, N], BF16, name="mg", tag="mg", bufs=2, align_bytes=64)
-            nc.scalar.copy(out=mg[i][:].rearrange("p (r t) -> p r t", t=4), in_=mt[i][:].rearrange("p t r -> p r t"))
+            eng_copy = nc.vector.tensor_copy if i < V_CM else nc.scalar.copy
+            eng_copy(out=mg[i][:].rearrange("p (r t) -> p r t", t=4), in_=mt[i][:].rearrange("p t r -> p r t"))
 
         def QM(i):
             mc[i] = work.tile([P, P], U32, name="mc", tag="mc", bufs=2, align_bytes=64)
@@ -276,7 +278,7 @@ def tile_mdn_module_pa_kernel(tc, h, W2, b2, x, y, eps, Wv, out_0, out_1):
             square_sum(ub["x"][:], ssx[:, k : k + 1])
 
         def VT(i):
-            tt[i] = work.tile([P, N], F32, name="tt", tag="tt", bufs=1)
+            tt[i] = work.tile([P, N], F32, name="tt", tag="tt", bufs=2)
             eng = nc.gpsimd if T_ON_GPSIMD else nc.vector
             eng.tensor_tensor(out=tt[i][:], in0=std[i][:], in1=eraw[i // 4][:, N * (i % 4) : N * (i % 4 + 1)], op=ALU.mult)
 
@@ -304,7 +306,7 @@ def tile_mdn_module_pa_kernel(tc, h, W2, b2, x, y, eps, Wv, out_0, out_1):
             nc.sync.dma_start(out=fx_v[:, i, :], in_=fx[:])
 
         def EE(i):
-            ee[i] = work.tile([P, N], F32, name="ee", tag="ee", bufs=2)
+            ee[i] = work.tile([P, N], F32, name="ee", tag="ee", bufs=3)
             nc.vector.tensor_tensor(out=ee[i][:], in0=nd[i][:], in1=istd[i][:], op=ALU.mult)
 
         def SQ(i):
@@ -332,8 +334,8 @@ def tile_mdn_module_pa_kernel(tc, h, W2, b2, x, y, eps, Wv, out_0, out_1):
         nc.vector.memset(brow[:], 0.0)
         nc.vector.memset(ones[:], 1.0)
         nc.scalar.dma_start(out=brow[0:1, :], in_=b2.rearrange("(o n) -> o n", o=1))
-        load_wv()
         load_x(0)
+        load_wv()
         load_x(1)
         load_w2(0)
         load_w2(1)
@@ -342,13 +344,14 @@ def tile_mdn_module_pa_kernel(tc, h, W2, b2, x, y, eps, Wv, out_0, out_1):
         load_x(3)
         load_h(0)
 
+        x_front(0)
         wvg = regroup(vcopy, w2raw["v"], slice(0, N), N, "wvg")
         quant(wvg, wvc[:], wvs[:])
-        x_front(0)
         x_quant(0)
         x_front(1)
         x_quant(1)
         x_back(0)
+        x_back(1)
         w2_rg(0, 0, vcopy)
         w2_rg(0, 1, vcopy)
         load_w2(3)
@@ -360,118 +363,89 @@ def tile_mdn_module_pa_kernel(tc, h, W2, b2, x, y, eps, Wv, out_0, out_1):
         load_ye(1)
         w2_q(0, 0)
         w2_q(0, 1)
-        x_back(1)
         x_front(2)
         w2_rg(1, 0, vcopy)
         w2_rg(1, 1, vcopy)
         w2_q(1, 0)
         w2_q(1, 1)
+        x_quant(2)
         x_front(3)
+        x_back(2)
         w2_rg(2, 0, vcopy)
-        w2_rg(2, 1, vcopy)
+        x_quant(3)
         w2_q(2, 0)
-        w2_q(2, 1)
+        TH(0)
+        CH(0, 0)
+        CH(0, 1)
+        x_back(3)
         for half in range(2):
             b_ps = psum.tile([P, N], F32, name="f", tag="f", bufs=3)
             nc.tensor.matmul(out=b_ps[:], lhsT=ones[:], rhs=brow[:, N * half : N * (half + 1)], start=True, stop=True)
             nc.scalar.copy(out=bias[:, N * half : N * (half + 1)], in_=b_ps[:])
-        TH(0)
-        CH(0, 0)
-        CH(0, 1)
         TH(1)
+        w2_rg(3, 0, vcopy)
+        w2_rg(2, 1, vcopy)
+        w2_q(3, 0)
 
-        xt = {}
-        for a in range(-3, NT + 3):
-            xk = 10 + 2 * a
+        for a in range(-3, NT + 4):
             if a >= 1 and a % 2 == 1 and (a + 7) // 2 < NT // 2:
                 load_h((a + 7) // 2)
             if a == 2:
                 load_ye(2)
             if a == 6:
                 load_ye(3)
-            if ok(a - 1):
-                SI(a - 1)
-            if 8 <= xk - 1 < NT:
-                SX(xk - 1)
+            if ok(a - 3):
+                SQ(a - 3)
             if ok(a + 4):
                 CH(a + 4, 0)
                 CH(a + 4, 1)
-            if a == -2:
-                wg["m"] = regroup(nc.scalar.copy, w2raw["m"], slice(0, N), N, "wmg")
             if ok(a + 1):
                 V1(a + 1)
-            if T_ON_GPSIMD and ok(a):
-                V2(a)
             if ok(a):
+                V2(a)
                 QM(a)
             if ok(a - 1):
                 T1(a - 1)
-            if ok(a) and not T_ON_GPSIMD:
-                V2(a)
-            if a == -3:
-                w2_rg(3, 0, vcopy)
-            if T_ON_GPSIMD and ok(a + 3):
+            if ok(a + 3):
                 QH(a + 3)
+            if a == -3:
+                w2_rg(3, 1, vcopy)
+                w2_q(2, 1)
+            if a == -2:
+                w2_q(3, 1)
+                for j in range(4):
+                    x_bvx(j)
+            if a == -1:
+                wg["m"] = regroup(vcopy, w2raw["m"], slice(0, N), N, "wmg")
             if ok(a - 1):
                 T2(a - 1)
-            if ok(a + 3) and not T_ON_GPSIMD:
-                QH(a + 3)
-            if a == -3:
-                w2_q(3, 0)
-            if a == -2:
-                w2_rg(3, 1, vcopy)
-                x_quant(2)
-                x_bvx(0)
-                x_bvx(1)
+            if ok(a - 2):
+                EE(a - 2)
             if a == -1:
-                w2_q(3, 1)
                 quant(wg["m"], wmc[:], wms[:])
-                x_quant(3)
-            if a == 2:
-                x_bvx(2)
-            if a == 4:
-                x_bvx(3)
-            if T_ON_GPSIMD:
-                if ok(a - 2):
-                    EE(a - 2)
-                if ok(a - 1):
-                    T3(a - 1)
-            else:
-                if ok(a - 1):
-                    T3(a - 1)
-                    VT(a - 1)
-                if ok(a - 2):
-                    EE(a - 2)
             if ok(a - 1):
+                T3(a - 1)
                 ND(a - 1)
                 FX(a - 1)
             if ok(a + 2):
                 MF(a + 2, 0)
-            elif ok(a + 1):
-                TM(a + 1)
-            if ok(a):
-                MU(a)
-            if 8 <= xk < NT:
-                UX(xk)
-            if ok(a + 2) and ok(a + 1):
-                TM(a + 1)
             if ok(a + 1):
                 MF(a + 1, 1)
             if ok(a):
+                MU(a)
+            if ok(a + 1):
+                TM(a + 1)
+            if ok(a + 5):
+                TH(a + 5)
+            if ok(a):
                 SD(a)
-                if T_ON_GPSIMD:
-                    VT(a)
-            if 8 <= xk < NT:
-                SX(xk)
-                UX(xk + 1)
+                VT(a)
+            if ok(a - 1):
+                SI(a - 1)
             if ok(a):
                 SU(a)
             if ok(a + 1):
                 CM(a + 1)
-            if ok(a - 2):
-                SQ(a - 2)
-            if ok(a + 5):
-                TH(a + 5)
 
         nc.vector.tensor_tensor(out=lp[:], in0=slv[:], in1=ssq[:], op=ALU.add)
         nc.vector.tensor_scalar(

@@ -22,7 +22,6 @@ FLOPS = 2 * B * H * 2 * N + 2 * 2 * B * N * N
 
 T_ON_GPSIMD = True
 S_HALVES = ()
-V_CM = 0
 
 
 def tile_mdn_module_pa_kernel(tc, h, W2, b2, x, y, eps, Wv, out_0, out_1):
@@ -225,14 +224,13 @@ def tile_mdn_module_pa_kernel(tc, h, W2, b2, x, y, eps, Wv, out_0, out_1):
             )
 
         def TM(i):
-            mt[i] = psum.tile([P, 4, P], F32, name="mt", tag="mt", bufs=2)
+            mt[i] = psum.tile([P, 4, P], F32, name="mt", tag="mt", bufs=1)
             for t in range(4):
                 nc.tensor.transpose(mt[i][:, t, :], mu[i][:, P * t : P * (t + 1)], ident[:])
 
         def CM(i):
             mg[i] = work.tile([P, N], BF16, name="mg", tag="mg", bufs=2, align_bytes=64)
-            eng_copy = nc.vector.tensor_copy if i < V_CM else nc.scalar.copy
-            eng_copy(out=mg[i][:].rearrange("p (r t) -> p r t", t=4), in_=mt[i][:].rearrange("p t r -> p r t"))
+            nc.scalar.copy(out=mg[i][:].rearrange("p (r t) -> p r t", t=4), in_=mt[i][:].rearrange("p t r -> p r t"))
 
         def QM(i):
             mc[i] = work.tile([P, P], U32, name="mc", tag="mc", bufs=2, align_bytes=64)
@@ -306,7 +304,7 @@ def tile_mdn_module_pa_kernel(tc, h, W2, b2, x, y, eps, Wv, out_0, out_1):
             nc.sync.dma_start(out=fx_v[:, i, :], in_=fx[:])
 
         def EE(i):
-            ee[i] = work.tile([P, N], F32, name="ee", tag="ee", bufs=3)
+            ee[i] = work.tile([P, N], F32, name="ee", tag="ee", bufs=2)
             nc.vector.tensor_tensor(out=ee[i][:], in0=nd[i][:], in1=istd[i][:], op=ALU.mult)
 
         def SQ(i):
@@ -334,8 +332,8 @@ def tile_mdn_module_pa_kernel(tc, h, W2, b2, x, y, eps, Wv, out_0, out_1):
         nc.vector.memset(brow[:], 0.0)
         nc.vector.memset(ones[:], 1.0)
         nc.scalar.dma_start(out=brow[0:1, :], in_=b2.rearrange("(o n) -> o n", o=1))
-        load_x(0)
         load_wv()
+        load_x(0)
         load_x(1)
         load_w2(0)
         load_w2(1)
@@ -344,14 +342,13 @@ def tile_mdn_module_pa_kernel(tc, h, W2, b2, x, y, eps, Wv, out_0, out_1):
         load_x(3)
         load_h(0)
 
-        x_front(0)
         wvg = regroup(vcopy, w2raw["v"], slice(0, N), N, "wvg")
         quant(wvg, wvc[:], wvs[:])
+        x_front(0)
         x_quant(0)
         x_front(1)
         x_quant(1)
         x_back(0)
-        x_back(1)
         w2_rg(0, 0, vcopy)
         w2_rg(0, 1, vcopy)
         load_w2(3)
@@ -363,89 +360,107 @@ def tile_mdn_module_pa_kernel(tc, h, W2, b2, x, y, eps, Wv, out_0, out_1):
         load_ye(1)
         w2_q(0, 0)
         w2_q(0, 1)
+        x_back(1)
         x_front(2)
         w2_rg(1, 0, vcopy)
         w2_rg(1, 1, vcopy)
         w2_q(1, 0)
         w2_q(1, 1)
-        x_quant(2)
         x_front(3)
-        x_back(2)
         w2_rg(2, 0, vcopy)
-        x_quant(3)
+        w2_rg(2, 1, vcopy)
         w2_q(2, 0)
-        TH(0)
-        CH(0, 0)
-        CH(0, 1)
-        x_back(3)
+        w2_q(2, 1)
         for half in range(2):
             b_ps = psum.tile([P, N], F32, name="f", tag="f", bufs=3)
             nc.tensor.matmul(out=b_ps[:], lhsT=ones[:], rhs=brow[:, N * half : N * (half + 1)], start=True, stop=True)
             nc.scalar.copy(out=bias[:, N * half : N * (half + 1)], in_=b_ps[:])
+        TH(0)
+        CH(0, 0)
+        CH(0, 1)
         TH(1)
-        w2_rg(3, 0, vcopy)
-        w2_rg(2, 1, vcopy)
-        w2_q(3, 0)
 
-        for a in range(-3, NT + 4):
+        xt = {}
+        for a in range(-3, NT + 3):
+            xk = 10 + 2 * a
             if a >= 1 and a % 2 == 1 and (a + 7) // 2 < NT // 2:
                 load_h((a + 7) // 2)
             if a == 2:
                 load_ye(2)
             if a == 6:
                 load_ye(3)
-            if ok(a - 3):
-                SQ(a - 3)
+            if ok(a - 1):
+                SI(a - 1)
+            if 8 <= xk - 1 < NT:
+                SX(xk - 1)
             if ok(a + 4):
                 CH(a + 4, 0)
                 CH(a + 4, 1)
+            if a == -2:
+                wg["m"] = regroup(nc.scalar.copy, w2raw["m"], slice(0, N), N, "wmg")
             if ok(a + 1):
                 V1(a + 1)
-            if ok(a):
-                V2(a)
-                QM(a)
             if ok(a - 1):
                 T1(a - 1)
+            if ok(a):
+                V2(a)
+            if ok(a - 1):
+                T2(a - 1)
+            if ok(a):
+                QM(a)
+            if ok(a - 1):
+                T3(a - 1)
+            if a == -3:
+                w2_rg(3, 0, vcopy)
             if ok(a + 3):
                 QH(a + 3)
             if a == -3:
-                w2_rg(3, 1, vcopy)
-                w2_q(2, 1)
+                w2_q(3, 0)
             if a == -2:
-                w2_q(3, 1)
-                for j in range(4):
-                    x_bvx(j)
+                w2_rg(3, 1, vcopy)
+                x_quant(2)
+                x_bvx(0)
+                x_bvx(1)
             if a == -1:
-                wg["m"] = regroup(vcopy, w2raw["m"], slice(0, N), N, "wmg")
-            if ok(a - 1):
-                T2(a - 1)
+                w2_q(3, 1)
+                quant(wg["m"], wmc[:], wms[:])
+                x_quant(3)
+            if a == 2:
+                x_bvx(2)
+            if a == 4:
+                x_bvx(3)
             if ok(a - 2):
                 EE(a - 2)
-            if a == -1:
-                quant(wg["m"], wmc[:], wms[:])
             if ok(a - 1):
-                T3(a - 1)
                 ND(a - 1)
                 FX(a - 1)
             if ok(a + 2):
                 MF(a + 2, 0)
+            elif ok(a + 1):
+                TM(a + 1)
+            if ok(a):
+                MU(a)
+            if 8 <= xk < NT:
+                UX(xk)
+            if ok(a + 2) and ok(a + 1):
+                TM(a + 1)
             if ok(a + 1):
                 MF(a + 1, 1)
             if ok(a):
-                MU(a)
-            if ok(a + 1):
-                TM(a + 1)
-            if ok(a + 5):
-                TH(a + 5)
-            if ok(a):
                 SD(a)
-                VT(a)
-            if ok(a - 1):
-                SI(a - 1)
+                if T_ON_GPSIMD:
+                    VT(a)
+            if 8 <= xk < NT:
+                SX(xk)
+                UX(xk + 1)
             if ok(a):
                 SU(a)
             if ok(a + 1):
                 CM(a + 1)
+            if ok(a - 2):
+                SQ(a - 2)
+            if ok(a + 5):
+                TH(a + 5)
 
         nc.vector.tensor_tensor(out=lp[:], in0=slv[:], in1=ssq[:], op=ALU.add)
         nc.vector.tensor_scalar(

@@ -54,6 +54,7 @@ def tile_mdn_module_pa_kernel(tc, h, W2, b2, x, y, eps, Wv, out_0, out_1):
         slv = keep.tile([P, NT], F32, name="slv", tag="slv")
         bvx = keep.tile([P, NT], F32, name="bvx", tag="bvx")
         lp = keep.tile([P, NT], F32, name="lp", tag="lp")
+        lpc = keep.tile([P, NT], F32, name="lpc", tag="lpc")
 
         w2raw = {}
         xraw = {}
@@ -332,8 +333,8 @@ def tile_mdn_module_pa_kernel(tc, h, W2, b2, x, y, eps, Wv, out_0, out_1):
         nc.vector.memset(brow[:], 0.0)
         nc.vector.memset(ones[:], 1.0)
         nc.scalar.dma_start(out=brow[0:1, :], in_=b2.rearrange("(o n) -> o n", o=1))
-        load_wv()
         load_x(0)
+        load_wv()
         load_x(1)
         load_w2(0)
         load_w2(1)
@@ -342,10 +343,10 @@ def tile_mdn_module_pa_kernel(tc, h, W2, b2, x, y, eps, Wv, out_0, out_1):
         load_x(3)
         load_h(0)
 
-        wvg = regroup(vcopy, w2raw["v"], slice(0, N), N, "wvg")
-        quant(wvg, wvc[:], wvs[:])
         x_front(0)
+        wvg = regroup(vcopy, w2raw["v"], slice(0, N), N, "wvg")
         x_quant(0)
+        quant(wvg, wvc[:], wvs[:])
         x_front(1)
         x_quant(1)
         x_back(0)
@@ -396,8 +397,6 @@ def tile_mdn_module_pa_kernel(tc, h, W2, b2, x, y, eps, Wv, out_0, out_1):
             if ok(a + 4):
                 CH(a + 4, 0)
                 CH(a + 4, 1)
-            if a == -2:
-                wg["m"] = regroup(nc.scalar.copy, w2raw["m"], slice(0, N), N, "wmg")
             if ok(a + 1):
                 V1(a + 1)
             if ok(a - 1):
@@ -422,15 +421,20 @@ def tile_mdn_module_pa_kernel(tc, h, W2, b2, x, y, eps, Wv, out_0, out_1):
                 x_bvx(0)
                 x_bvx(1)
             if a == -1:
+                wg["m"] = regroup(vcopy, w2raw["m"], slice(0, N), N, "wmg")
                 w2_q(3, 1)
-                quant(wg["m"], wmc[:], wms[:])
                 x_quant(3)
+                quant(wg["m"], wmc[:], wms[:])
             if a == 2:
                 x_bvx(2)
             if a == 4:
                 x_bvx(3)
             if ok(a - 2):
                 EE(a - 2)
+            if a == NT:
+                nc.vector.tensor_scalar(
+                    out=lpc[:], in0=slv[:], scalar1=-0.5, scalar2=-0.5 * N * math.log(2.0 * math.pi), op0=ALU.mult, op1=ALU.add
+                )
             if ok(a - 1):
                 ND(a - 1)
                 FX(a - 1)
@@ -462,8 +466,5 @@ def tile_mdn_module_pa_kernel(tc, h, W2, b2, x, y, eps, Wv, out_0, out_1):
             if ok(a + 5):
                 TH(a + 5)
 
-        nc.vector.tensor_tensor(out=lp[:], in0=slv[:], in1=ssq[:], op=ALU.add)
-        nc.vector.tensor_scalar(
-            out=lp[:], in0=lp[:], scalar1=-0.5, scalar2=-0.5 * N * math.log(2.0 * math.pi), op0=ALU.mult, op1=ALU.add
-        )
+        nc.vector.scalar_tensor_tensor(out=lp[:], in0=ssq[:], scalar=-0.5, in1=lpc[:], op0=ALU.mult, op1=ALU.add)
         nc.sync.dma_start(out=lp_v, in_=lp[:])

@@ -19,9 +19,17 @@ N = 512
 NT = B // P
 KP = H // 512
 FLOPS = 2 * B * H * 2 * N + 2 * 2 * B * N * N
-
-T_ON_GPSIMD = True
-S_HALVES = ()
+NCAST = 11
+T_G = False
+VT_V = (15,)
+HCB = 4
+MUB = 4
+A0 = -2
+QH0 = 1
+CH0 = 2
+TH0 = 2
+NCAST = 12
+T_G = True
 
 
 def tile_mdn_module_pa_kernel(tc, h, W2, b2, x, y, eps, Wv, out_0, out_1):
@@ -46,8 +54,6 @@ def tile_mdn_module_pa_kernel(tc, h, W2, b2, x, y, eps, Wv, out_0, out_1):
         w2s = keep.tile([P, KP * 2 * N], U8, name="w2s", tag="w2s", align_bytes=64)
         wvc = keep.tile([P, N], U32, name="wvc", tag="wvc", align_bytes=64)
         wvs = keep.tile([P, N], U8, name="wvs", tag="wvs", align_bytes=64)
-        wmc = keep.tile([P, N], U32, name="wmc", tag="wmc", align_bytes=64)
-        wms = keep.tile([P, N], U8, name="wms", tag="wms", align_bytes=64)
         ssx = keep.tile([P, NT], F32, name="ssx", tag="ssx")
         ssm = keep.tile([P, NT], F32, name="ssm", tag="ssm")
         ssq = keep.tile([P, NT], F32, name="ssq", tag="ssq")
@@ -55,6 +61,7 @@ def tile_mdn_module_pa_kernel(tc, h, W2, b2, x, y, eps, Wv, out_0, out_1):
         bvx = keep.tile([P, NT], F32, name="bvx", tag="bvx")
         lp = keep.tile([P, NT], F32, name="lp", tag="lp")
         lpc = keep.tile([P, NT], F32, name="lpc", tag="lpc")
+        neg = keep.tile([P, 1], F32, name="neg", tag="neg")
 
         w2raw = {}
         xraw = {}
@@ -71,6 +78,7 @@ def tile_mdn_module_pa_kernel(tc, h, W2, b2, x, y, eps, Wv, out_0, out_1):
         fmu = {}
         flv = {}
         mu = {}
+        mub = {}
         lv = {}
         std = {}
         istd = {}
@@ -82,8 +90,8 @@ def tile_mdn_module_pa_kernel(tc, h, W2, b2, x, y, eps, Wv, out_0, out_1):
         mc = {}
         ms = {}
         ub = {}
-        cc = {}
         sm = {}
+        wg = {}
 
         def load_w2(g):
             w2raw[g] = work.tile([P, 4 * 2 * N], BF16, name="w2raw", tag="w2raw", bufs=3)
@@ -99,13 +107,10 @@ def tile_mdn_module_pa_kernel(tc, h, W2, b2, x, y, eps, Wv, out_0, out_1):
                 in_=Wv.rearrange("(u q e) c -> q u (e c)", u=2, e=2),
             )
 
-        def load_wm():
-            w2raw["m"] = keep.tile([P, 4 * N], BF16, name="wmraw", tag="wmraw")
-            nc.sync.dma_start(out=w2raw["m"][:].rearrange("p (t c) -> p t c", t=4), in_=Wv.rearrange("(t p) c -> p t c", t=4))
-
-        def load_x(j):
-            xraw[j] = work.tile([P, 4 * N], BF16, name="xraw", tag="xraw", bufs=4)
-            nc.sync.dma_start(out=xraw[j][:].rearrange("p (i n) -> p i n", i=4), in_=x_v[:, 4 * j : 4 * j + 4, :])
+        def load_x(j, lo=0, hi=4):
+            if lo == 0:
+                xraw[j] = work.tile([P, 4 * N], BF16, name="xraw", tag="xraw", bufs=4)
+            nc.sync.dma_start(out=xraw[j][:, N * lo : N * hi].rearrange("p (i n) -> p i n", i=hi - lo), in_=x_v[:, 4 * j + lo : 4 * j + hi, :])
 
         def load_h(j):
             hraw[j] = work.tile([P, 2 * H], BF16, name="hraw", tag="hraw", bufs=4)
@@ -117,9 +122,9 @@ def tile_mdn_module_pa_kernel(tc, h, W2, b2, x, y, eps, Wv, out_0, out_1):
             yraw[j] = work.tile([P, 4 * N], BF16, name="yraw", tag="yraw", bufs=3)
             nc.sync.dma_start(out=yraw[j][:].rearrange("p (i n) -> p i n", i=4), in_=y_v[:, 4 * j : 4 * j + 4, :])
 
-        def regroup(eng_copy, raw, cols, width, name):
-            g_t = work.tile([P, 4 * width], BF16, name=name, tag="wgrp", bufs=4, align_bytes=64)
-            eng_copy(
+        def regroup(raw, cols, name):
+            g_t = work.tile([P, 4 * N], BF16, name=name, tag="wgrp", bufs=4, align_bytes=64)
+            nc.vector.tensor_copy(
                 out=g_t[:].rearrange("p (c i t) -> p c t i", i=4, t=4),
                 in_=raw[:].rearrange("p (t n) -> p t n", t=4)[:, :, cols].rearrange("p t (c i) -> p c t i", i=4),
             )
@@ -128,26 +133,40 @@ def tile_mdn_module_pa_kernel(tc, h, W2, b2, x, y, eps, Wv, out_0, out_1):
         def quant(g_t, codes, scales):
             nc.vector.quantize_mx(out=codes.bitcast(FP8X4), scales=scales, in_=g_t[:])
 
-        def x_transposes(j, pr, tag="tr", bufs=2):
-            t_ps = psum.tile([P, 4, P], F32, name=tag, tag=tag, bufs=bufs)
+        def WR(g, half):
+            wg[(g, half)] = regroup(w2raw[g], slice(N * half, N * (half + 1)), "w2g")
+
+        def WQ(g, half):
+            o = 2 * N * g + N * half
+            quant(wg[(g, half)], w2c[:, o : o + N], w2s[:, o : o + N])
+
+        def VR():
+            wg["v"] = regroup(w2raw["v"], slice(0, N), "wvg")
+
+        def VQ():
+            quant(wg["v"], wvc[:], wvs[:])
+
+        def XT(j, pr):
+            t_ps = psum.tile([P, 4, P], F32, name="tr", tag="tr", bufs=2)
             xw = xraw[j][:].bitcast(F32)
             for q in range(4):
                 nc.tensor.transpose(t_ps[:, q, :], xw[:, 512 * pr + 128 * q : 512 * pr + 128 * (q + 1)], ident[:])
-            return t_ps
-
-        def x_copy(j, pr, t_ps):
             if pr == 0:
                 xg[j] = work.tile([P, 4 * N], BF16, name="xg", tag="xg", bufs=2, align_bytes=64)
             dst = xg[j][:].bitcast(F32).rearrange("p (i r u) -> p i r u", i=4, u=2)
             nc.scalar.copy(out=dst[:, 2 * pr : 2 * pr + 2, :, :], in_=t_ps[:].rearrange("p (i u) r -> p i r u", u=2))
 
-        def x_quant(j):
+        def XQ(j):
             xc[j] = keep.tile([P, N], U32, name="xc%d" % j, tag="xc%d" % j, align_bytes=64)
             xs[j] = keep.tile([P, N], U8, name="xs%d" % j, tag="xs%d" % j, align_bytes=64)
             quant(xg[j], xc[j][:], xs[j][:])
 
-        def x_matmul(i):
-            u_ps = psum.tile([P, N], F32, name="f", tag="f", bufs=3)
+        def square_sum(src, acc):
+            junk = work.tile([P, N], BF16, name="junk", tag="junk", bufs=2)
+            nc.scalar.activation(out=junk[:], in_=src, func=ACT.Square, accum_out=acc)
+
+        def XM(i, tag, bufs):
+            u_ps = psum.tile([P, N], F32, name=tag, tag=tag, bufs=bufs)
             j = i // 4
             r = i % 4
             nc.tensor.matmul_mx(
@@ -161,17 +180,13 @@ def tile_mdn_module_pa_kernel(tc, h, W2, b2, x, y, eps, Wv, out_0, out_1):
             )
             return u_ps
 
-        def square_sum(src, acc):
-            junk = work.tile([P, N], BF16, name="junk", tag="junk", bufs=2)
-            nc.scalar.activation(out=junk[:], in_=src, func=ACT.Square, accum_out=acc)
+        def XS(i, u_ps):
+            square_sum(u_ps[:], ssx[:, i : i + 1])
 
-        def x_bvx(j):
+        def XB(j):
             nc.vector.tensor_scalar(
                 out=bvx[:, 4 * j : 4 * j + 4], in0=ssx[:, 4 * j : 4 * j + 4], scalar1=1e-3, scalar2=0.99, op0=ALU.add, op1=ALU.mult
             )
-
-        def ok(i):
-            return 0 <= i < NT
 
         def TH(i):
             hw = hraw[i // 2][:].bitcast(F32)
@@ -191,8 +206,8 @@ def tile_mdn_module_pa_kernel(tc, h, W2, b2, x, y, eps, Wv, out_0, out_1):
             nc.scalar.copy(out=dst[:, 2 * b : 2 * b + 2, :, :], in_=trb[i][b][:].rearrange("p (g u) r -> p g r u", u=2))
 
         def QH(i):
-            hc[i] = work.tile([P, N], U32, name="hc", tag="hc", bufs=4, align_bytes=64)
-            hs[i] = work.tile([P, N], U8, name="hs", tag="hs", bufs=4, align_bytes=64)
+            hc[i] = work.tile([P, N], U32, name="hc", tag="hc", bufs=HCB, align_bytes=64)
+            hs[i] = work.tile([P, N], U8, name="hs", tag="hs", bufs=HCB, align_bytes=64)
             quant(hg[i], hc[i][:], hs[i][:])
 
         def MF(i, half):
@@ -201,37 +216,50 @@ def tile_mdn_module_pa_kernel(tc, h, W2, b2, x, y, eps, Wv, out_0, out_1):
                 fmu[i] = acc
             else:
                 flv[i] = acc
-            if True:
-                for g in range(KP):
-                    o = 2 * N * g + N * half
-                    nc.tensor.matmul_mx(
-                        out=acc[:],
-                        lhsT=hc[i][:, P * g : P * (g + 1)].bitcast(FP8X4),
-                        lhsT_scale=hs[i][:, P * g : P * (g + 1)],
-                        rhs=w2c[:, o : o + N].bitcast(FP8X4),
-                        rhs_scale=w2s[:, o : o + N],
-                        start=(g == 0),
-                        stop=(g == KP - 1),
-                    )
+            for g in range(KP):
+                o = 2 * N * g + N * half
+                nc.tensor.matmul_mx(
+                    out=acc[:],
+                    lhsT=hc[i][:, P * g : P * (g + 1)].bitcast(FP8X4),
+                    lhsT_scale=hs[i][:, P * g : P * (g + 1)],
+                    rhs=w2c[:, o : o + N].bitcast(FP8X4),
+                    rhs_scale=w2s[:, o : o + N],
+                    start=(g == 0),
+                    stop=(g == KP - 1),
+                )
 
         def V1(i):
-            mu[i] = work.tile([P, N], F32, name="mu", tag="mu", bufs=4)
+            mu[i] = work.tile([P, N], F32, name="mu", tag="mu", bufs=MUB)
             nc.vector.tensor_tensor(out=mu[i][:], in0=fmu[i][:], in1=bias[:, 0:N], op=ALU.add)
 
+        def MB(i):
+            if i < NCAST:
+                mub[i] = work.tile([P, N], BF16, name="mub", tag="mub", bufs=2, align_bytes=64)
+                nc.vector.tensor_copy(out=mub[i][:], in_=mu[i][:])
+
         def V2(i):
-            lv[i] = work.tile([P, N], F32, name="lv", tag="lv", bufs=3)
+            lv[i] = work.tile([P, N], F32, name="lv", tag="lv", bufs=2)
             nc.vector.scalar_tensor_tensor(
                 out=lv[i][:], in0=flv[i][:], scalar=1.0, in1=bias[:, N : 2 * N], op0=ALU.mult, op1=ALU.add, accum_out=slv[:, i : i + 1]
             )
 
         def TM(i):
             mt[i] = psum.tile([P, 4, P], F32, name="mt", tag="mt", bufs=1)
-            for t in range(4):
-                nc.tensor.transpose(mt[i][:, t, :], mu[i][:, P * t : P * (t + 1)], ident[:])
+            if i < NCAST:
+                mw = mub[i][:].bitcast(F32)
+                for u in range(2):
+                    nc.tensor.transpose(mt[i][:, u, :], mw[:, P * u : P * (u + 1)], ident[:])
+            else:
+                for t in range(4):
+                    o = 256 * (t // 2) + t % 2
+                    nc.tensor.transpose(mt[i][:, t, :], mu[i][:, o : o + 255 : 2], ident[:])
 
         def CM(i):
             mg[i] = work.tile([P, N], BF16, name="mg", tag="mg", bufs=2, align_bytes=64)
-            nc.scalar.copy(out=mg[i][:].rearrange("p (r t) -> p r t", t=4), in_=mt[i][:].rearrange("p t r -> p r t"))
+            if i < NCAST:
+                nc.scalar.copy(out=mg[i][:].bitcast(F32).rearrange("p (r u) -> p r u", u=2), in_=mt[i][:, 0:2, :].rearrange("p u r -> p r u"))
+            else:
+                nc.scalar.copy(out=mg[i][:].rearrange("p (r t) -> p r t", t=4), in_=mt[i][:].rearrange("p t r -> p r t"))
 
         def QM(i):
             mc[i] = work.tile([P, P], U32, name="mc", tag="mc", bufs=2, align_bytes=64)
@@ -239,13 +267,13 @@ def tile_mdn_module_pa_kernel(tc, h, W2, b2, x, y, eps, Wv, out_0, out_1):
             quant(mg[i], mc[i][:], ms[i][:])
 
         def MU(i):
-            ub[i] = psum.tile([P, N], F32, name="u", tag="u", bufs=1)
+            ub[i] = psum.tile([P, N], F32, name="u", tag="u", bufs=2)
             nc.tensor.matmul_mx(
                 out=ub[i][:],
                 lhsT=mc[i][:].bitcast(FP8X4),
                 lhsT_scale=ms[i][:],
-                rhs=wmc[:].bitcast(FP8X4),
-                rhs_scale=wms[:],
+                rhs=wvc[:].bitcast(FP8X4),
+                rhs_scale=wvs[:],
                 start=True,
                 stop=True,
             )
@@ -258,40 +286,31 @@ def tile_mdn_module_pa_kernel(tc, h, W2, b2, x, y, eps, Wv, out_0, out_1):
             nc.scalar.activation(out=std[i][:], in_=lv[i][:], func=ACT.Exp, scale=0.5)
 
         def SI(i):
-            istd[i] = work.tile([P, N], F32, name="istd", tag="istd", bufs=3)
+            istd[i] = work.tile([P, N], F32, name="istd", tag="istd", bufs=2)
             nc.scalar.activation(out=istd[i][:], in_=lv[i][:], func=ACT.Exp, scale=-0.5)
 
-        def UX(k):
-            ub["x"] = psum.tile([P, N], F32, name="ux", tag="ux", bufs=1)
-            nc.tensor.matmul_mx(
-                out=ub["x"][:],
-                lhsT=xc[k // 4][:, P * (k % 4) : P * (k % 4 + 1)].bitcast(FP8X4),
-                lhsT_scale=xs[k // 4][:, P * (k % 4) : P * (k % 4 + 1)],
-                rhs=wvc[:].bitcast(FP8X4),
-                rhs_scale=wvs[:],
-                start=True,
-                stop=True,
-            )
-
-        def SX(k):
-            square_sum(ub["x"][:], ssx[:, k : k + 1])
-
         def VT(i):
-            tt[i] = work.tile([P, N], F32, name="tt", tag="tt", bufs=2)
-            eng = nc.gpsimd if T_ON_GPSIMD else nc.vector
+            tt[i] = work.tile([P, N], F32, name="tt", tag="tt", bufs=1)
+            eng = nc.vector if i in VT_V else nc.gpsimd
             eng.tensor_tensor(out=tt[i][:], in0=std[i][:], in1=eraw[i // 4][:, N * (i % 4) : N * (i % 4 + 1)], op=ALU.mult)
 
         def T1(i):
             sm[i] = work.tile([P, 4], F32, name="sm", tag="sm", bufs=4)
-            nc.vector.tensor_scalar(
+            (nc.gpsimd if T_G else nc.vector).tensor_scalar(
                 out=sm[i][:, 0:1], in0=ssm[:, i : i + 1], scalar1=1e-3, scalar2=bvx[:, i : i + 1], op0=ALU.add, op1=ALU.max
             )
 
         def T2(i):
-            nc.vector.reciprocal(out=sm[i][:, 1:2], in_=sm[i][:, 0:1])
+            if T_G:
+                nc.gpsimd.tensor_tensor(out=sm[i][:, 1:2], in0=sm[i][:, 0:1], in1=neg[:], op=ALU.pow)
+            else:
+                nc.vector.reciprocal(out=sm[i][:, 1:2], in_=sm[i][:, 0:1])
 
         def T3(i):
-            nc.vector.tensor_scalar(out=sm[i][:, 2:3], in0=sm[i][:, 1:2], scalar1=bvx[:, i : i + 1], scalar2=None, op0=ALU.mult)
+            if T_G:
+                nc.gpsimd.tensor_tensor(out=sm[i][:, 2:3], in0=sm[i][:, 1:2], in1=bvx[:, i : i + 1], op=ALU.mult)
+            else:
+                nc.vector.tensor_scalar(out=sm[i][:, 2:3], in0=sm[i][:, 1:2], scalar1=bvx[:, i : i + 1], scalar2=None, op0=ALU.mult)
 
         def ND(i):
             nd[i] = work.tile([P, N], F32, name="nd", tag="nd", bufs=2)
@@ -300,7 +319,7 @@ def tile_mdn_module_pa_kernel(tc, h, W2, b2, x, y, eps, Wv, out_0, out_1):
             )
 
         def FX(i):
-            fx = work.tile([P, N], F32, name="fx", tag="fx", bufs=3)
+            fx = work.tile([P, N], F32, name="fx", tag="fx", bufs=2)
             nc.vector.scalar_tensor_tensor(out=fx[:], in0=mu[i][:], scalar=sm[i][:, 2:3], in1=tt[i][:], op0=ALU.mult, op1=ALU.add)
             nc.sync.dma_start(out=fx_v[:, i, :], in_=fx[:])
 
@@ -311,160 +330,149 @@ def tile_mdn_module_pa_kernel(tc, h, W2, b2, x, y, eps, Wv, out_0, out_1):
         def SQ(i):
             square_sum(ee[i][:], ssq[:, i : i + 1])
 
-        def x_front(j):
-            for pr in range(2):
-                x_copy(j, pr, x_transposes(j, pr))
-
-        def x_back(j):
+        def XX(j, tags=("f", "f", "f", "f")):
             for i in range(4 * j, 4 * j + 4):
-                square_sum(x_matmul(i)[:], ssx[:, i : i + 1])
+                XS(i, XM(i, "f", 3))
 
-        def w2_rg(g, half, eng_copy):
-            wg[(g, half)] = regroup(eng_copy, w2raw[g], slice(N * half, N * (half + 1)), N, "w2g")
-
-        def w2_q(g, half):
-            o = 2 * N * g + N * half
-            quant(wg[(g, half)], w2c[:, o : o + N], w2s[:, o : o + N])
-
-        wg = {}
-        vcopy = nc.vector.tensor_copy
         brow = keep.tile([P, 2 * N], BF16, name="brow", tag="brow")
         ones = keep.tile([P, P], BF16, name="ones", tag="ones")
         nc.vector.memset(brow[:], 0.0)
         nc.vector.memset(ones[:], 1.0)
-        nc.scalar.dma_start(out=brow[0:1, :], in_=b2.rearrange("(o n) -> o n", o=1))
-        load_x(0)
+        nc.vector.memset(neg[:], -1.0)
+        def load_hh(i):
+            if i % 2 == 0:
+                hraw[i // 2] = work.tile([P, 2 * H], BF16, name="hraw", tag="hraw", bufs=4)
+            nc.sync.dma_start(out=hraw[i // 2][:, H * (i % 2) : H * (i % 2 + 1)], in_=h_v[:, i, :])
+        load_x(0, 0, 2)
         load_wv()
-        load_x(1)
+        load_x(0, 2, 4)
+        nc.sync.dma_start(out=brow[0:1, :], in_=b2.rearrange("(o n) -> o n", o=1))
         load_w2(0)
+        load_x(1)
         load_w2(1)
         load_x(2)
         load_w2(2)
+        load_hh(0)
         load_x(3)
-        load_h(0)
-
-        x_front(0)
-        wvg = regroup(vcopy, w2raw["v"], slice(0, N), N, "wvg")
-        x_quant(0)
-        quant(wvg, wvc[:], wvs[:])
-        x_front(1)
-        x_quant(1)
-        x_back(0)
-        w2_rg(0, 0, vcopy)
-        w2_rg(0, 1, vcopy)
-        load_w2(3)
-        load_h(1)
-        load_wm()
-        load_ye(0)
-        load_h(2)
-        load_h(3)
-        load_ye(1)
-        w2_q(0, 0)
-        w2_q(0, 1)
-        x_back(1)
-        x_front(2)
-        w2_rg(1, 0, vcopy)
-        w2_rg(1, 1, vcopy)
-        w2_q(1, 0)
-        w2_q(1, 1)
-        x_front(3)
-        w2_rg(2, 0, vcopy)
-        w2_rg(2, 1, vcopy)
-        w2_q(2, 0)
-        w2_q(2, 1)
+        XT(0, 0)
+        XT(0, 1)
+        VR()
+        XQ(0)
+        VQ()
         for half in range(2):
-            b_ps = psum.tile([P, N], F32, name="f", tag="f", bufs=3)
+            b_ps = psum.tile([P, N], F32, name="u", tag="u", bufs=2)
             nc.tensor.matmul(out=b_ps[:], lhsT=ones[:], rhs=brow[:, N * half : N * (half + 1)], start=True, stop=True)
             nc.scalar.copy(out=bias[:, N * half : N * (half + 1)], in_=b_ps[:])
+        WR(0, 0)
+        XX(0)
+        XT(1, 0)
+        XT(1, 1)
+        WR(0, 1)
+        WQ(0, 0)
+        WQ(0, 1)
+        load_w2(3)
+        load_hh(1)
+        load_h(1)
+        load_ye(0)
+        XQ(1)
+        XT(2, 0)
+        XT(2, 1)
+        XX(1)
+        WR(1, 0)
+        WR(1, 1)
+        WQ(1, 0)
+        WQ(1, 1)
+        XQ(2)
         TH(0)
         CH(0, 0)
         CH(0, 1)
+        WR(2, 0)
+        XT(3, 0)
+        XT(3, 1)
+        WR(2, 1)
+        WQ(2, 0)
+        WQ(2, 1)
         TH(1)
-
-        xt = {}
-        for a in range(-3, NT + 3):
-            xk = 10 + 2 * a
+        CH(1, 0)
+        CH(1, 1)
+        XX(2)
+        QH(0)
+        WR(3, 0)
+        XQ(3)
+        WQ(3, 0)
+        TH(2)
+        CH(2, 0)
+        CH(2, 1)
+        WR(3, 1)
+        QH(1)
+        EXTRA = {-2: (lambda: load_h(2),lambda: load_ye(1)), -1: (lambda: load_h(3),)}
+        EXV = {-2: (lambda: WQ(3, 1),), 0:(lambda:XB(0),lambda:XB(1),lambda:XB(2),), 6:(lambda:XB(3),)}
+        XSTEP = {-1: (12,), 0: (13,), 1: (14,), 2: (15,)}
+        ux = {}
+        def ok(i):
+            return 0 <= i < NT
+        for a in range(A0, NT + 2):
+            for f in EXTRA.get(a, ()):
+                f()
             if a >= 1 and a % 2 == 1 and (a + 7) // 2 < NT // 2:
                 load_h((a + 7) // 2)
             if a == 2:
                 load_ye(2)
             if a == 6:
                 load_ye(3)
-            if ok(a - 1):
-                SI(a - 1)
-            if 8 <= xk - 1 < NT:
-                SX(xk - 1)
-            if ok(a + 4):
-                CH(a + 4, 0)
-                CH(a + 4, 1)
             if ok(a + 1):
                 V1(a + 1)
-            if ok(a - 1):
-                T1(a - 1)
             if ok(a):
                 V2(a)
             if ok(a - 1):
-                T2(a - 1)
-            if ok(a):
-                QM(a)
-            if ok(a - 1):
-                T3(a - 1)
-            if a == -3:
-                w2_rg(3, 0, vcopy)
-            if ok(a + 3):
+                VT(a - 1)
+            if ok(a + 1):
+                MB(a + 1)
+            if ok(a + 3) and a + 3 > QH0:
                 QH(a + 3)
-            if a == -3:
-                w2_q(3, 0)
-            if a == -2:
-                w2_rg(3, 1, vcopy)
-                x_quant(2)
-                x_bvx(0)
-                x_bvx(1)
-            if a == -1:
-                wg["m"] = regroup(vcopy, w2raw["m"], slice(0, N), N, "wmg")
-                w2_q(3, 1)
-                x_quant(3)
-                quant(wg["m"], wmc[:], wms[:])
-            if a == 2:
-                x_bvx(2)
-            if a == 4:
-                x_bvx(3)
-            if ok(a - 2):
-                EE(a - 2)
-            if a == NT:
-                nc.vector.tensor_scalar(
-                    out=lpc[:], in0=slv[:], scalar1=-0.5, scalar2=-0.5 * N * math.log(2.0 * math.pi), op0=ALU.mult, op1=ALU.add
-                )
             if ok(a - 1):
                 ND(a - 1)
-                FX(a - 1)
-            if ok(a + 2):
-                MF(a + 2, 0)
-            elif ok(a + 1):
-                TM(a + 1)
+                if a < NT:
+                    FX(a - 1)
+                    EE(a - 1)
+                else:
+                    EE(a - 1)
+                    FX(a - 1)
+            for f in EXV.get(a, ()):
+                f()
             if ok(a):
                 MU(a)
-            if 8 <= xk < NT:
-                UX(xk)
-            if ok(a + 2) and ok(a + 1):
-                TM(a + 1)
+            if ok(a + 2):
+                MF(a + 2, 0)
             if ok(a + 1):
+                TM(a + 1)
                 MF(a + 1, 1)
-            if ok(a):
-                SD(a)
-                if T_ON_GPSIMD:
-                    VT(a)
-            if 8 <= xk < NT:
-                SX(xk)
-                UX(xk + 1)
+            for k in XSTEP.get(a, ()):
+                ux[k] = XM(k, "u", 2)
+            if ok(a + 4) and a + 4 > CH0:
+                CH(a + 4, 0)
+                CH(a + 4, 1)
             if ok(a):
                 SU(a)
             if ok(a + 1):
                 CM(a + 1)
+            if ok(a):
+                SD(a)
+                SI(a)
+            for k in XSTEP.get(a, ()):
+                XS(k, ux[k])
+            if ok(a):
+                T1(a)
+                T2(a)
+                T3(a)
             if ok(a - 2):
                 SQ(a - 2)
-            if ok(a + 5):
+            if ok(a + 1):
+                QM(a + 1)
+            if ok(a + 5) and a + 5 > TH0:
                 TH(a + 5)
-
+        nc.vector.tensor_scalar(
+            out=lpc[:], in0=slv[:], scalar1=-0.5, scalar2=-0.5 * N * math.log(2.0 * math.pi), op0=ALU.mult, op1=ALU.add
+        )
         nc.vector.scalar_tensor_tensor(out=lp[:], in0=ssq[:], scalar=-0.5, in1=lpc[:], op0=ALU.mult, op1=ALU.add)
         nc.sync.dma_start(out=lp_v, in_=lp[:])

@@ -19,7 +19,7 @@ N = 512
 NT = B // P
 KP = H // 512
 FLOPS = 2 * B * H * 2 * N + 2 * 2 * B * N * N
-NCAST = 11
+CAST = tuple(range(11))
 T_G = False
 VT_V = (15,)
 HCB = 4
@@ -28,8 +28,8 @@ A0 = -2
 QH0 = 1
 CH0 = 2
 TH0 = 2
-NCAST = 12
-T_G = True
+CAST = tuple(range(12))
+T_G = False
 
 
 def tile_mdn_module_pa_kernel(tc, h, W2, b2, x, y, eps, Wv, out_0, out_1):
@@ -233,7 +233,7 @@ def tile_mdn_module_pa_kernel(tc, h, W2, b2, x, y, eps, Wv, out_0, out_1):
             nc.vector.tensor_tensor(out=mu[i][:], in0=fmu[i][:], in1=bias[:, 0:N], op=ALU.add)
 
         def MB(i):
-            if i < NCAST:
+            if i in CAST:
                 mub[i] = work.tile([P, N], BF16, name="mub", tag="mub", bufs=2, align_bytes=64)
                 nc.vector.tensor_copy(out=mub[i][:], in_=mu[i][:])
 
@@ -245,7 +245,7 @@ def tile_mdn_module_pa_kernel(tc, h, W2, b2, x, y, eps, Wv, out_0, out_1):
 
         def TM(i):
             mt[i] = psum.tile([P, 4, P], F32, name="mt", tag="mt", bufs=1)
-            if i < NCAST:
+            if i in CAST:
                 mw = mub[i][:].bitcast(F32)
                 for u in range(2):
                     nc.tensor.transpose(mt[i][:, u, :], mw[:, P * u : P * (u + 1)], ident[:])
@@ -256,7 +256,7 @@ def tile_mdn_module_pa_kernel(tc, h, W2, b2, x, y, eps, Wv, out_0, out_1):
 
         def CM(i):
             mg[i] = work.tile([P, N], BF16, name="mg", tag="mg", bufs=2, align_bytes=64)
-            if i < NCAST:
+            if i in CAST:
                 nc.scalar.copy(out=mg[i][:].bitcast(F32).rearrange("p (r u) -> p r u", u=2), in_=mt[i][:, 0:2, :].rearrange("p u r -> p r u"))
             else:
                 nc.scalar.copy(out=mg[i][:].rearrange("p (r t) -> p r t", t=4), in_=mt[i][:].rearrange("p t r -> p r t"))
@@ -422,12 +422,17 @@ def tile_mdn_module_pa_kernel(tc, h, W2, b2, x, y, eps, Wv, out_0, out_1):
                 load_ye(3)
             if ok(a + 1):
                 V1(a + 1)
+            if ok(a - 1):
+                T1(a - 1)
             if ok(a):
                 V2(a)
             if ok(a - 1):
                 VT(a - 1)
+                T2(a - 1)
             if ok(a + 1):
                 MB(a + 1)
+            if ok(a - 1):
+                T3(a - 1)
             if ok(a + 3) and a + 3 > QH0:
                 QH(a + 3)
             if ok(a - 1):
@@ -461,10 +466,6 @@ def tile_mdn_module_pa_kernel(tc, h, W2, b2, x, y, eps, Wv, out_0, out_1):
                 SI(a)
             for k in XSTEP.get(a, ()):
                 XS(k, ux[k])
-            if ok(a):
-                T1(a)
-                T2(a)
-                T3(a)
             if ok(a - 2):
                 SQ(a - 2)
             if ok(a + 1):

@@ -21,15 +21,35 @@ KP = H // 512
 FLOPS = 2 * B * H * 2 * N + 2 * 2 * B * N * N
 CAST = tuple(range(11))
 T_G = False
+PERM = False
+PO = False
+ISB = 3
+STB = 2
+E = 1
+TO = -1
+TT = -1
+LM = 1
+LD = 7
+HLD = 3
+THX = {}
+T3S = False
 VT_V = (15,)
 HCB = 4
 MUB = 4
-A0 = -2
-QH0 = 1
+LM = 1
+LD = 7
+HLD = 3
+QH0 = 0
 CH0 = 2
 TH0 = 2
 CAST = tuple(range(12))
 T_G = False
+T3S = True
+PO = False
+E = 1
+TT = -1
+STB = 2
+ISB = 2
 
 
 def tile_mdn_module_pa_kernel(tc, h, W2, b2, x, y, eps, Wv, out_0, out_1):
@@ -129,6 +149,14 @@ def tile_mdn_module_pa_kernel(tc, h, W2, b2, x, y, eps, Wv, out_0, out_1):
                 in_=raw[:].rearrange("p (t n) -> p t n", t=4)[:, :, cols].rearrange("p t (c i) -> p c t i", i=4),
             )
             return g_t
+
+        def SR(g, half):
+            g_t = work.tile([P, 4 * N], BF16, name="w2g", tag="wgrp", bufs=4, align_bytes=64)
+            nc.scalar.copy(
+                out=g_t[:].rearrange("p (c i t) -> p c t i", i=4, t=4),
+                in_=w2raw[g][:].rearrange("p (t n) -> p t n", t=4)[:, :, slice(N * half, N * (half + 1))].rearrange("p t (c i) -> p c t i", i=4),
+            )
+            wg[(g, half)] = g_t
 
         def quant(g_t, codes, scales):
             nc.vector.quantize_mx(out=codes.bitcast(FP8X4), scales=scales, in_=g_t[:])
@@ -252,7 +280,7 @@ def tile_mdn_module_pa_kernel(tc, h, W2, b2, x, y, eps, Wv, out_0, out_1):
             else:
                 for t in range(4):
                     o = 256 * (t // 2) + t % 2
-                    nc.tensor.transpose(mt[i][:, t, :], mu[i][:, o : o + 255 : 2], ident[:])
+                    nc.tensor.transpose(mt[i][:, t, :], mu[i][:, P * t : P * (t + 1)] if PERM else mu[i][:, o : o + 255 : 2], ident[:])
 
         def CM(i):
             mg[i] = work.tile([P, N], BF16, name="mg", tag="mg", bufs=2, align_bytes=64)
@@ -282,11 +310,11 @@ def tile_mdn_module_pa_kernel(tc, h, W2, b2, x, y, eps, Wv, out_0, out_1):
             square_sum(ub[i][:], ssm[:, i : i + 1])
 
         def SD(i):
-            std[i] = work.tile([P, N], F32, name="std", tag="std", bufs=2)
+            std[i] = work.tile([P, N], F32, name="std", tag="std", bufs=STB)
             nc.scalar.activation(out=std[i][:], in_=lv[i][:], func=ACT.Exp, scale=0.5)
 
         def SI(i):
-            istd[i] = work.tile([P, N], F32, name="istd", tag="istd", bufs=2)
+            istd[i] = work.tile([P, N], F32, name="istd", tag="istd", bufs=ISB)
             nc.scalar.activation(out=istd[i][:], in_=lv[i][:], func=ACT.Exp, scale=-0.5)
 
         def VT(i):
@@ -306,11 +334,14 @@ def tile_mdn_module_pa_kernel(tc, h, W2, b2, x, y, eps, Wv, out_0, out_1):
             else:
                 nc.vector.reciprocal(out=sm[i][:, 1:2], in_=sm[i][:, 0:1])
 
-        def T3(i):
+        def T3(i, on_s=False):
             if T_G:
                 nc.gpsimd.tensor_tensor(out=sm[i][:, 2:3], in0=sm[i][:, 1:2], in1=bvx[:, i : i + 1], op=ALU.mult)
             else:
-                nc.vector.tensor_scalar(out=sm[i][:, 2:3], in0=sm[i][:, 1:2], scalar1=bvx[:, i : i + 1], scalar2=None, op0=ALU.mult)
+                if on_s:
+                    nc.scalar.activation(out=sm[i][:, 2:3], in_=sm[i][:, 1:2], func=ACT.Copy, scale=bvx[:, i : i + 1])
+                else:
+                    nc.vector.tensor_scalar(out=sm[i][:, 2:3], in0=sm[i][:, 1:2], scalar1=bvx[:, i : i + 1], scalar2=None, op0=ALU.mult)
 
         def ND(i):
             nd[i] = work.tile([P, N], F32, name="nd", tag="nd", bufs=2)
@@ -334,6 +365,8 @@ def tile_mdn_module_pa_kernel(tc, h, W2, b2, x, y, eps, Wv, out_0, out_1):
             for i in range(4 * j, 4 * j + 4):
                 XS(i, XM(i, "f", 3))
 
+        EXU = {}
+        EXP = {}
         brow = keep.tile([P, 2 * N], BF16, name="brow", tag="brow")
         ones = keep.tile([P, P], BF16, name="ones", tag="ones")
         nc.vector.memset(brow[:], 0.0)
@@ -357,16 +390,16 @@ def tile_mdn_module_pa_kernel(tc, h, W2, b2, x, y, eps, Wv, out_0, out_1):
         XT(0, 0)
         XT(0, 1)
         VR()
-        XQ(0)
         VQ()
+        XQ(0)
         for half in range(2):
             b_ps = psum.tile([P, N], F32, name="u", tag="u", bufs=2)
             nc.tensor.matmul(out=b_ps[:], lhsT=ones[:], rhs=brow[:, N * half : N * (half + 1)], start=True, stop=True)
             nc.scalar.copy(out=bias[:, N * half : N * (half + 1)], in_=b_ps[:])
         WR(0, 0)
-        XX(0)
         XT(1, 0)
         XT(1, 1)
+        XX(0)
         WR(0, 1)
         WQ(0, 0)
         WQ(0, 1)
@@ -392,63 +425,60 @@ def tile_mdn_module_pa_kernel(tc, h, W2, b2, x, y, eps, Wv, out_0, out_1):
         WR(2, 1)
         WQ(2, 0)
         WQ(2, 1)
+        XX(2)
         TH(1)
         CH(1, 0)
         CH(1, 1)
-        XX(2)
         QH(0)
         WR(3, 0)
-        XQ(3)
-        WQ(3, 0)
         TH(2)
         CH(2, 0)
         CH(2, 1)
-        WR(3, 1)
-        QH(1)
+        WQ(3, 0)
         EXTRA = {-2: (lambda: load_h(2),lambda: load_ye(1)), -1: (lambda: load_h(3),)}
-        EXV = {-2: (lambda: WQ(3, 1),), 0:(lambda:XB(0),lambda:XB(1),lambda:XB(2),), 6:(lambda:XB(3),)}
-        XSTEP = {-1: (12,), 0: (13,), 1: (14,), 2: (15,)}
+        EXU = {-1: (lambda: WQ(3, 1),), 0: (lambda: XQ(3),)}
+        EXV = {-2: (lambda: WR(3, 1),), 0:(lambda:XB(0),lambda:XB(1),lambda:XB(2),), 9:(lambda:XB(3),)}
+        XSTEP = {1: (12,), 3: (13,), 5: (14,), 7: (15,)}
         ux = {}
         def ok(i):
             return 0 <= i < NT
-        for a in range(A0, NT + 2):
+        for a in range(-2, NT + 2):
             for f in EXTRA.get(a, ()):
                 f()
-            if a >= 1 and a % 2 == 1 and (a + 7) // 2 < NT // 2:
-                load_h((a + 7) // 2)
+            if (a + LD) % 2 == 0 and HLD < (a + LD) // 2 < NT // 2:
+                load_h((a + LD) // 2)
             if a == 2:
                 load_ye(2)
             if a == 6:
                 load_ye(3)
+            if ok(a - 1):
+                T1(a - 1)
             if ok(a + 1):
                 V1(a + 1)
             if ok(a - 1):
-                T1(a - 1)
+                T2(a - 1)
+            for f in EXU.get(a, ()):
+                f()
             if ok(a):
                 V2(a)
             if ok(a - 1):
                 VT(a - 1)
-                T2(a - 1)
+            if ok(a - 1) and (a + 3 >= NT or not T3S):
+                T3(a - 1)
+            if ok(a):
+                QM(a)
             if ok(a + 1):
                 MB(a + 1)
-            if ok(a - 1):
-                T3(a - 1)
             if ok(a + 3) and a + 3 > QH0:
                 QH(a + 3)
-            if ok(a - 1):
-                ND(a - 1)
-                if a < NT:
-                    FX(a - 1)
-                    EE(a - 1)
-                else:
-                    EE(a - 1)
-                    FX(a - 1)
             for f in EXV.get(a, ()):
+                f()
+            if ok(a + 2):
+                MF(a + 2, 0)
+            for f in EXP.get(a, ()):
                 f()
             if ok(a):
                 MU(a)
-            if ok(a + 2):
-                MF(a + 2, 0)
             if ok(a + 1):
                 TM(a + 1)
                 MF(a + 1, 1)
@@ -457,21 +487,32 @@ def tile_mdn_module_pa_kernel(tc, h, W2, b2, x, y, eps, Wv, out_0, out_1):
             if ok(a + 4) and a + 4 > CH0:
                 CH(a + 4, 0)
                 CH(a + 4, 1)
+            if ok(a - 1) and T3S and a + 3 < NT:
+                T3(a - 1, True)
+            if ok(a + 5) and a + 5 > TH0:
+                TH(a + 5)
+            if ok(a):
+                SD(a)
+            if ok(a - 2) and a + 4 < NT:
+                SQ(a - 2)
             if ok(a):
                 SU(a)
+            if ok(a - 2) and a + 4 >= NT:
+                SQ(a - 2)
             if ok(a + 1):
                 CM(a + 1)
             if ok(a):
-                SD(a)
                 SI(a)
             for k in XSTEP.get(a, ()):
                 XS(k, ux[k])
-            if ok(a - 2):
-                SQ(a - 2)
-            if ok(a + 1):
-                QM(a + 1)
-            if ok(a + 5) and a + 5 > TH0:
-                TH(a + 5)
+            if ok(a - 1):
+                ND(a - 1)
+                if a < NT:
+                    FX(a - 1)
+                    EE(a - 1)
+                else:
+                    EE(a - 1)
+                    FX(a - 1)
         nc.vector.tensor_scalar(
             out=lpc[:], in0=slv[:], scalar1=-0.5, scalar2=-0.5 * N * math.log(2.0 * math.pi), op0=ALU.mult, op1=ALU.add
         )

@@ -40,16 +40,16 @@ LM = 1
 LD = 7
 HLD = 3
 QH0 = 0
-CH0 = 2
-TH0 = 2
+CH0 = 1
+TH0 = 1
 CAST = tuple(range(12))
 T_G = False
-T3S = True
+T3S = False
 PO = False
 E = 1
 TT = -1
 STB = 2
-ISB = 2
+ISB = 3
 
 
 def tile_mdn_module_pa_kernel(tc, h, W2, b2, x, y, eps, Wv, out_0, out_1):
@@ -431,9 +431,6 @@ def tile_mdn_module_pa_kernel(tc, h, W2, b2, x, y, eps, Wv, out_0, out_1):
         CH(1, 1)
         QH(0)
         WR(3, 0)
-        TH(2)
-        CH(2, 0)
-        CH(2, 1)
         WQ(3, 0)
         EXTRA = {-2: (lambda: load_h(2),lambda: load_ye(1)), -1: (lambda: load_h(3),)}
         EXU = {-1: (lambda: WQ(3, 1),), 0: (lambda: XQ(3),)}
@@ -442,7 +439,7 @@ def tile_mdn_module_pa_kernel(tc, h, W2, b2, x, y, eps, Wv, out_0, out_1):
         ux = {}
         def ok(i):
             return 0 <= i < NT
-        for a in range(-2, NT + 2):
+        for a in range(-2, NT + 1):
             for f in EXTRA.get(a, ()):
                 f()
             if (a + LD) % 2 == 0 and HLD < (a + LD) // 2 < NT // 2:
@@ -451,68 +448,68 @@ def tile_mdn_module_pa_kernel(tc, h, W2, b2, x, y, eps, Wv, out_0, out_1):
                 load_ye(2)
             if a == 6:
                 load_ye(3)
-            if ok(a - 1):
-                T1(a - 1)
             if ok(a + 1):
                 V1(a + 1)
-            if ok(a - 1):
-                T2(a - 1)
             for f in EXU.get(a, ()):
                 f()
             if ok(a):
                 V2(a)
             if ok(a - 1):
                 VT(a - 1)
-            if ok(a - 1) and (a + 3 >= NT or not T3S):
+                T1(a - 1)
+            if ok(a + 1):
+                MB(a + 1)
+            if ok(a - 1):
+                T2(a - 1)
+            for f in EXV.get(a, ()):
+                f()
+            if ok(a - 2):
+                EE(a - 2)
+            if ok(a - 1):
                 T3(a - 1)
             if ok(a):
                 QM(a)
-            if ok(a + 1):
-                MB(a + 1)
-            if ok(a + 3) and a + 3 > QH0:
-                QH(a + 3)
-            for f in EXV.get(a, ()):
-                f()
             if ok(a + 2):
                 MF(a + 2, 0)
             for f in EXP.get(a, ()):
                 f()
+            if PO and ok(a + 1):
+                TM(a + 1)
+            if ok(a + 1):
+                MF(a + 1, 1)
             if ok(a):
                 MU(a)
-            if ok(a + 1):
-                TM(a + 1)
-                MF(a + 1, 1)
             for k in XSTEP.get(a, ()):
                 ux[k] = XM(k, "u", 2)
-            if ok(a + 4) and a + 4 > CH0:
-                CH(a + 4, 0)
-                CH(a + 4, 1)
-            if ok(a - 1) and T3S and a + 3 < NT:
-                T3(a - 1, True)
-            if ok(a + 5) and a + 5 > TH0:
-                TH(a + 5)
+            if not PO and ok(a + 1):
+                TM(a + 1)
+            if ok(a + 3) and a + 3 > CH0:
+                CH(a + 3, 0)
+                CH(a + 3, 1)
+            if ok(a + 4) and a + 4 > TH0:
+                TH(a + 4)
             if ok(a):
                 SD(a)
-            if ok(a - 2) and a + 4 < NT:
+                SI(a)
+            if ok(a - 2):
                 SQ(a - 2)
-            if ok(a):
-                SU(a)
-            if ok(a - 2) and a + 4 >= NT:
-                SQ(a - 2)
-            if ok(a + 1):
+            if PO and ok(a + 1):
                 CM(a + 1)
             if ok(a):
-                SI(a)
+                SU(a)
+            if not PO and ok(a + 1):
+                CM(a + 1)
             for k in XSTEP.get(a, ()):
                 XS(k, ux[k])
             if ok(a - 1):
                 ND(a - 1)
-                if a < NT:
-                    FX(a - 1)
-                    EE(a - 1)
-                else:
-                    EE(a - 1)
-                    FX(a - 1)
+            if a == NT:
+                EE(a - 1)
+                SQ(a - 1)
+            if ok(a - 1):
+                FX(a - 1)
+            if ok(a + 3) and a + 3 > QH0:
+                QH(a + 3)
         nc.vector.tensor_scalar(
             out=lpc[:], in0=slv[:], scalar1=-0.5, scalar2=-0.5 * N * math.log(2.0 * math.pi), op0=ALU.mult, op1=ALU.add
         )

@@ -33,6 +33,11 @@ LD = 7
 HLD = 3
 THX = {}
 T3S = False
+TP = False
+EE_G = ()
+CHV = ()
+NDB = 2
+TTB = 1
 VT_V = (15,)
 HCB = 4
 MUB = 4
@@ -42,7 +47,7 @@ HLD = 3
 QH0 = 0
 CH0 = 1
 TH0 = 1
-CAST = tuple(range(12))
+CAST = tuple(range(16))
 T_G = False
 T3S = False
 PO = False
@@ -50,6 +55,7 @@ E = 1
 TT = -1
 STB = 2
 ISB = 3
+MUF = True
 
 
 def tile_mdn_module_pa_kernel(tc, h, W2, b2, x, y, eps, Wv, out_0, out_1):
@@ -216,6 +222,9 @@ def tile_mdn_module_pa_kernel(tc, h, W2, b2, x, y, eps, Wv, out_0, out_1):
                 out=bvx[:, 4 * j : 4 * j + 4], in0=ssx[:, 4 * j : 4 * j + 4], scalar1=1e-3, scalar2=0.99, op0=ALU.add, op1=ALU.mult
             )
 
+        def XBS(j, n=1):
+            nc.scalar.activation(out=bvx[:, 4 * j : 4 * (j + n)], in_=ssx[:, 4 * j : 4 * (j + n)], func=ACT.Copy, scale=0.99, bias=0.99e-3)
+
         def TH(i):
             hw = hraw[i // 2][:].bitcast(F32)
             base = 1024 * (i % 2)
@@ -231,7 +240,7 @@ def tile_mdn_module_pa_kernel(tc, h, W2, b2, x, y, eps, Wv, out_0, out_1):
             if b == 0:
                 hg[i] = work.tile([P, H], BF16, name="hg", tag="hg", bufs=2, align_bytes=64)
             dst = hg[i][:].bitcast(F32).rearrange("p (g r u) -> p g r u", g=4, u=2)
-            nc.scalar.copy(out=dst[:, 2 * b : 2 * b + 2, :, :], in_=trb[i][b][:].rearrange("p (g u) r -> p g r u", u=2))
+            (nc.vector.tensor_copy if (i, b) in CHV else nc.scalar.copy)(out=dst[:, 2 * b : 2 * b + 2, :, :], in_=trb[i][b][:].rearrange("p (g u) r -> p g r u", u=2))
 
         def QH(i):
             hc[i] = work.tile([P, N], U32, name="hc", tag="hc", bufs=HCB, align_bytes=64)
@@ -318,7 +327,7 @@ def tile_mdn_module_pa_kernel(tc, h, W2, b2, x, y, eps, Wv, out_0, out_1):
             nc.scalar.activation(out=istd[i][:], in_=lv[i][:], func=ACT.Exp, scale=-0.5)
 
         def VT(i):
-            tt[i] = work.tile([P, N], F32, name="tt", tag="tt", bufs=1)
+            tt[i] = work.tile([P, N], F32, name="tt", tag="tt", bufs=TTB)
             eng = nc.vector if i in VT_V else nc.gpsimd
             eng.tensor_tensor(out=tt[i][:], in0=std[i][:], in1=eraw[i // 4][:, N * (i % 4) : N * (i % 4 + 1)], op=ALU.mult)
 
@@ -343,20 +352,37 @@ def tile_mdn_module_pa_kernel(tc, h, W2, b2, x, y, eps, Wv, out_0, out_1):
                 else:
                     nc.vector.tensor_scalar(out=sm[i][:, 2:3], in0=sm[i][:, 1:2], scalar1=bvx[:, i : i + 1], scalar2=None, op0=ALU.mult)
 
-        def ND(i):
-            nd[i] = work.tile([P, N], F32, name="nd", tag="nd", bufs=2)
+        def TP1(i):
+            sm[i] = work.tile([P, 8], F32, name="sm", tag="sm", bufs=3)
             nc.vector.scalar_tensor_tensor(
-                out=nd[i][:], in0=mu[i][:], scalar=sm[i][:, 2:3], in1=yraw[i // 4][:, N * (i % 4) : N * (i % 4 + 1)], op0=ALU.mult, op1=ALU.subtract
+                out=sm[i][:, 0:2], in0=ssm[:, i : i + 2], scalar=1e-3, in1=bvx[:, i : i + 2], op0=ALU.add, op1=ALU.max
+            )
+
+        def TP2(i):
+            nc.vector.reciprocal(out=sm[i][:, 2:4], in_=sm[i][:, 0:2])
+
+        def TP3(i):
+            nc.vector.tensor_tensor(out=sm[i][:, 4:6], in0=sm[i][:, 2:4], in1=bvx[:, i : i + 2], op=ALU.mult)
+
+        def SC(i):
+            if TP:
+                return sm[i - i % 2][:, 4 + i % 2 : 5 + i % 2]
+            return sm[i][:, 2:3]
+
+        def ND(i):
+            nd[i] = work.tile([P, N], F32, name="nd", tag="nd", bufs=NDB)
+            nc.vector.scalar_tensor_tensor(
+                out=nd[i][:], in0=mu[i][:], scalar=SC(i), in1=yraw[i // 4][:, N * (i % 4) : N * (i % 4 + 1)], op0=ALU.mult, op1=ALU.subtract
             )
 
         def FX(i):
             fx = work.tile([P, N], F32, name="fx", tag="fx", bufs=2)
-            nc.vector.scalar_tensor_tensor(out=fx[:], in0=mu[i][:], scalar=sm[i][:, 2:3], in1=tt[i][:], op0=ALU.mult, op1=ALU.add)
+            nc.vector.scalar_tensor_tensor(out=fx[:], in0=mu[i][:], scalar=SC(i), in1=tt[i][:], op0=ALU.mult, op1=ALU.add)
             nc.sync.dma_start(out=fx_v[:, i, :], in_=fx[:])
 
         def EE(i):
             ee[i] = work.tile([P, N], F32, name="ee", tag="ee", bufs=2)
-            nc.vector.tensor_tensor(out=ee[i][:], in0=nd[i][:], in1=istd[i][:], op=ALU.mult)
+            (nc.gpsimd if i in EE_G else nc.vector).tensor_tensor(out=ee[i][:], in0=nd[i][:], in1=istd[i][:], op=ALU.mult)
 
         def SQ(i):
             square_sum(ee[i][:], ssq[:, i : i + 1])
@@ -369,8 +395,8 @@ def tile_mdn_module_pa_kernel(tc, h, W2, b2, x, y, eps, Wv, out_0, out_1):
         EXP = {}
         brow = keep.tile([P, 2 * N], BF16, name="brow", tag="brow")
         ones = keep.tile([P, P], BF16, name="ones", tag="ones")
-        nc.vector.memset(brow[:], 0.0)
-        nc.vector.memset(ones[:], 1.0)
+        nc.gpsimd.memset(brow[:], 0.0)
+        nc.gpsimd.memset(ones[:], 1.0)
         nc.vector.memset(neg[:], -1.0)
         def load_hh(i):
             if i % 2 == 0:
@@ -434,8 +460,8 @@ def tile_mdn_module_pa_kernel(tc, h, W2, b2, x, y, eps, Wv, out_0, out_1):
         WQ(3, 0)
         EXTRA = {-2: (lambda: load_h(2),lambda: load_ye(1)), -1: (lambda: load_h(3),)}
         EXU = {-1: (lambda: WQ(3, 1),), 0: (lambda: XQ(3),)}
-        EXV = {-2: (lambda: WR(3, 1),), 0:(lambda:XB(0),lambda:XB(1),lambda:XB(2),), 9:(lambda:XB(3),)}
-        XSTEP = {1: (12,), 3: (13,), 5: (14,), 7: (15,)}
+        EXV = {-2: (lambda: WR(3, 1),), 0: (lambda: XBS(0, 3),), 9: (lambda: XBS(3),)}
+        XSTEP = {2: (12,), 4: (13,), 6: (14,), 8: (15,)}
         ux = {}
         def ok(i):
             return 0 <= i < NT
@@ -448,57 +474,54 @@ def tile_mdn_module_pa_kernel(tc, h, W2, b2, x, y, eps, Wv, out_0, out_1):
                 load_ye(2)
             if a == 6:
                 load_ye(3)
+            if ok(a):
+                CM(a)
+            if ok(a + 3) and a + 3 > CH0:
+                CH(a + 3, 0)
+                CH(a + 3, 1)
             if ok(a + 1):
                 V1(a + 1)
+            if ok(a - 1):
+                T1(a - 1)
             for f in EXU.get(a, ()):
                 f()
             if ok(a):
                 V2(a)
             if ok(a - 1):
                 VT(a - 1)
-                T1(a - 1)
+                T2(a - 1)
             if ok(a + 1):
                 MB(a + 1)
-            if ok(a - 1):
-                T2(a - 1)
-            for f in EXV.get(a, ()):
-                f()
-            if ok(a - 2):
-                EE(a - 2)
-            if ok(a - 1):
-                T3(a - 1)
             if ok(a):
                 QM(a)
+            for f in EXV.get(a, ()):
+                f()
+            if ok(a - 1):
+                T3(a - 1)
+            if ok(a - 2):
+                EE(a - 2)
             if ok(a + 2):
                 MF(a + 2, 0)
             for f in EXP.get(a, ()):
                 f()
-            if PO and ok(a + 1):
-                TM(a + 1)
+            if MUF and ok(a):
+                MU(a)
             if ok(a + 1):
                 MF(a + 1, 1)
-            if ok(a):
+            if not MUF and ok(a):
                 MU(a)
             for k in XSTEP.get(a, ()):
                 ux[k] = XM(k, "u", 2)
-            if not PO and ok(a + 1):
+            if ok(a + 1):
                 TM(a + 1)
-            if ok(a + 3) and a + 3 > CH0:
-                CH(a + 3, 0)
-                CH(a + 3, 1)
             if ok(a + 4) and a + 4 > TH0:
                 TH(a + 4)
             if ok(a):
                 SD(a)
                 SI(a)
+                SU(a)
             if ok(a - 2):
                 SQ(a - 2)
-            if PO and ok(a + 1):
-                CM(a + 1)
-            if ok(a):
-                SU(a)
-            if not PO and ok(a + 1):
-                CM(a + 1)
             for k in XSTEP.get(a, ()):
                 XS(k, ux[k])
             if ok(a - 1):

from contextlib import ExitStack
import math

import concourse.mybir as mybir
from concourse.masks import make_identity

F32 = mybir.dt.float32
BF16 = mybir.dt.bfloat16
U32 = mybir.dt.uint32
U8 = mybir.dt.uint8
FP8X4 = mybir.dt.float8_e4m3fn_x4
ALU = mybir.AluOpType
ACT = mybir.ActivationFunctionType

P = 128
B = 2048
H = 2048
N = 512
NT = B // P
KP = H // 512
FLOPS = 2 * B * H * 2 * N + 2 * 2 * B * N * N
CAST = tuple(range(11))
T_G = False
PERM = False
PO = False
ISB = 3
STB = 2
E = 1
TO = -1
TT = -1
LM = 1
LD = 7
HLD = 3
THX = {}
T3S = False
TP = False
EE_G = ()
CHV = ()
NDB = 2
TTB = 1
VT_V = (15,)
HCB = 4
MUB = 4
LM = 1
LD = 7
HLD = 3
QH0 = 0
CH0 = 1
TH0 = 1
CAST = tuple(range(16))
T_G = False
T3S = False
PO = False
E = 1
TT = -1
STB = 2
ISB = 3
MUF = True


def tile_mdn_module_pa_kernel(tc, h, W2, b2, x, y, eps, Wv, out_0, out_1):
    nc = tc.nc
    h_v = h.rearrange("(p i) k -> p i k", i=NT)
    x_v = x.rearrange("(p i) n -> p i n", i=NT)
    y_v = y.rearrange("(p i) o n -> p i (o n)", i=NT)
    e_v = eps.rearrange("(p i) o n -> p i (o n)", i=NT)
    fx_v = out_0.rearrange("(p i) o n -> p i (o n)", i=NT)
    lp_v = out_1.rearrange("(p i) o -> p (i o)", i=NT)

    with ExitStack() as ctx:
        keep = ctx.enter_context(tc.tile_pool(name="keep", bufs=1))
        work = ctx.enter_context(tc.tile_pool(name="work", bufs=2))
        psum = ctx.enter_context(tc.psum_pool(name="psum", bufs=1))
        ctx.enter_context(tc.manual_schedule())

        ident = keep.tile([P, P], F32, name="ident", tag="ident")
        make_identity(nc, ident[:])
        bias = keep.tile([P, 2 * N], BF16, name="bias", tag="bias")
        w2c = keep.tile([P, KP * 2 * N], U32, name="w2c", tag="w2c", align_bytes=64)
        w2s = keep.tile([P, KP * 2 * N], U8, name="w2s", tag="w2s", align_bytes=64)
        wvc = keep.tile([P, N], U32, name="wvc", tag="wvc", align_bytes=64)
        wvs = keep.tile([P, N], U8, name="wvs", tag="wvs", align_bytes=64)
        ssx = keep.tile([P, NT], F32, name="ssx", tag="ssx")
        ssm = keep.tile([P, NT], F32, name="ssm", tag="ssm")
        ssq = keep.tile([P, NT], F32, name="ssq", tag="ssq")
        slv = keep.tile([P, NT], F32, name="slv", tag="slv")
        bvx = keep.tile([P, NT], F32, name="bvx", tag="bvx")
        lp = keep.tile([P, NT], F32, name="lp", tag="lp")
        lpc = keep.tile([P, NT], F32, name="lpc", tag="lpc")
        neg = keep.tile([P, 1], F32, name="neg", tag="neg")

        w2raw = {}
        xraw = {}
        hraw = {}
        yraw = {}
        eraw = {}
        xc = {}
        xs = {}
        xg = {}
        hg = {}
        hc = {}
        hs = {}
        trb = {}
        fmu = {}
        flv = {}
        mu = {}
        mub = {}
        lv = {}
        std = {}
        istd = {}
        tt = {}
        nd = {}
        ee = {}
        mt = {}
        mg = {}
        mc = {}
        ms = {}
        ub = {}
        sm = {}
        wg = {}

        def load_w2(g):
            w2raw[g] = work.tile([P, 4 * 2 * N], BF16, name="w2raw", tag="w2raw", bufs=3)
            nc.sync.dma_start(
                out=w2raw[g][:].rearrange("p (u z) -> p u z", u=2),
                in_=W2[512 * g : 512 * (g + 1), :].rearrange("(u q e) c -> q u (e c)", u=2, e=2),
            )

        def load_wv():
            w2raw["v"] = keep.tile([P, 4 * N], BF16, name="wvraw", tag="wvraw")
            nc.sync.dma_start(
                out=w2raw["v"][:].rearrange("p (u z) -> p u z", u=2),
                in_=Wv.rearrange("(u q e) c -> q u (e c)", u=2, e=2),
            )

        def load_x(j, lo=0, hi=4):
            if lo == 0:
                xraw[j] = work.tile([P, 4 * N], BF16, name="xraw", tag="xraw", bufs=4)
            nc.sync.dma_start(out=xraw[j][:, N * lo : N * hi].rearrange("p (i n) -> p i n", i=hi - lo), in_=x_v[:, 4 * j + lo : 4 * j + hi, :])

        def load_h(j):
            hraw[j] = work.tile([P, 2 * H], BF16, name="hraw", tag="hraw", bufs=4)
            nc.sync.dma_start(out=hraw[j][:].rearrange("p (i k) -> p i k", i=2), in_=h_v[:, 2 * j : 2 * j + 2, :])

        def load_ye(j):
            eraw[j] = work.tile([P, 4 * N], BF16, name="eraw", tag="eraw", bufs=3)
            nc.sync.dma_start(out=eraw[j][:].rearrange("p (i n) -> p i n", i=4), in_=e_v[:, 4 * j : 4 * j + 4, :])
            yraw[j] = work.tile([P, 4 * N], BF16, name="yraw", tag="yraw", bufs=3)
            nc.sync.dma_start(out=yraw[j][:].rearrange("p (i n) -> p i n", i=4), in_=y_v[:, 4 * j : 4 * j + 4, :])

        def regroup(raw, cols, name):
            g_t = work.tile([P, 4 * N], BF16, name=name, tag="wgrp", bufs=4, align_bytes=64)
            nc.vector.tensor_copy(
                out=g_t[:].rearrange("p (c i t) -> p c t i", i=4, t=4),
                in_=raw[:].rearrange("p (t n) -> p t n", t=4)[:, :, cols].rearrange("p t (c i) -> p c t i", i=4),
            )
            return g_t

        def SR(g, half):
            g_t = work.tile([P, 4 * N], BF16, name="w2g", tag="wgrp", bufs=4, align_bytes=64)
            nc.scalar.copy(
                out=g_t[:].rearrange("p (c i t) -> p c t i", i=4, t=4),
                in_=w2raw[g][:].rearrange("p (t n) -> p t n", t=4)[:, :, slice(N * half, N * (half + 1))].rearrange("p t (c i) -> p c t i", i=4),
            )
            wg[(g, half)] = g_t

        def quant(g_t, codes, scales):
            nc.vector.quantize_mx(out=codes.bitcast(FP8X4), scales=scales, in_=g_t[:])

        def WR(g, half):
            wg[(g, half)] = regroup(w2raw[g], slice(N * half, N * (half + 1)), "w2g")

        def WQ(g, half):
            o = 2 * N * g + N * half
            quant(wg[(g, half)], w2c[:, o : o + N], w2s[:, o : o + N])

        def VR():
            wg["v"] = regroup(w2raw["v"], slice(0, N), "wvg")

        def VQ():
            quant(wg["v"], wvc[:], wvs[:])

        def XT(j, pr):
            t_ps = psum.tile([P, 4, P], F32, name="tr", tag="tr", bufs=2)
            xw = xraw[j][:].bitcast(F32)
            for q in range(4):
                nc.tensor.transpose(t_ps[:, q, :], xw[:, 512 * pr + 128 * q : 512 * pr + 128 * (q + 1)], ident[:])
            if pr == 0:
                xg[j] = work.tile([P, 4 * N], BF16, name="xg", tag="xg", bufs=2, align_bytes=64)
            dst = xg[j][:].bitcast(F32).rearrange("p (i r u) -> p i r u", i=4, u=2)
            nc.scalar.copy(out=dst[:, 2 * pr : 2 * pr + 2, :, :], in_=t_ps[:].rearrange("p (i u) r -> p i r u", u=2))

        def XQ(j):
            xc[j] = keep.tile([P, N], U32, name="xc%d" % j, tag="xc%d" % j, align_bytes=64)
            xs[j] = keep.tile([P, N], U8, name="xs%d" % j, tag="xs%d" % j, align_bytes=64)
            quant(xg[j], xc[j][:], xs[j][:])

        def square_sum(src, acc):
            junk = work.tile([P, N], BF16, name="junk", tag="junk", bufs=2)
            nc.scalar.activation(out=junk[:], in_=src, func=ACT.Square, accum_out=acc)

        def XM(i, tag, bufs):
            u_ps = psum.tile([P, N], F32, name=tag, tag=tag, bufs=bufs)
            j = i // 4
            r = i % 4
            nc.tensor.matmul_mx(
                out=u_ps[:],
                lhsT=xc[j][:, P * r : P * (r + 1)].bitcast(FP8X4),
                lhsT_scale=xs[j][:, P * r : P * (r + 1)],
                rhs=wvc[:].bitcast(FP8X4),
                rhs_scale=wvs[:],
                start=True,
                stop=True,
            )
            return u_ps

        def XS(i, u_ps):
            square_sum(u_ps[:], ssx[:, i : i + 1])

        def XB(j):
            nc.vector.tensor_scalar(
                out=bvx[:, 4 * j : 4 * j + 4], in0=ssx[:, 4 * j : 4 * j + 4], scalar1=1e-3, scalar2=0.99, op0=ALU.add, op1=ALU.mult
            )

        def XBS(j, n=1):
            nc.scalar.activation(out=bvx[:, 4 * j : 4 * (j + n)], in_=ssx[:, 4 * j : 4 * (j + n)], func=ACT.Copy, scale=0.99, bias=0.99e-3)

        def TH(i):
            hw = hraw[i // 2][:].bitcast(F32)
            base = 1024 * (i % 2)
            trb[i] = []
            for b in range(2):
                t_ps = psum.tile([P, 4, P], F32, name="tr", tag="tr", bufs=2)
                for q in range(4):
                    o = base + 512 * b + 128 * q
                    nc.tensor.transpose(t_ps[:, q, :], hw[:, o : o + 128], ident[:])
                trb[i].append(t_ps)

        def CH(i, b):
            if b == 0:
                hg[i] = work.tile([P, H], BF16, name="hg", tag="hg", bufs=2, align_bytes=64)
            dst = hg[i][:].bitcast(F32).rearrange("p (g r u) -> p g r u", g=4, u=2)
            (nc.vector.tensor_copy if (i, b) in CHV else nc.scalar.copy)(out=dst[:, 2 * b : 2 * b + 2, :, :], in_=trb[i][b][:].rearrange("p (g u) r -> p g r u", u=2))

        def QH(i):
            hc[i] = work.tile([P, N], U32, name="hc", tag="hc", bufs=HCB, align_bytes=64)
            hs[i] = work.tile([P, N], U8, name="hs", tag="hs", bufs=HCB, align_bytes=64)
            quant(hg[i], hc[i][:], hs[i][:])

        def MF(i, half):
            acc = psum.tile([P, N], F32, name="f", tag="f", bufs=3)
            if half == 0:
                fmu[i] = acc
            else:
                flv[i] = acc
            for g in range(KP):
                o = 2 * N * g + N * half
                nc.tensor.matmul_mx(
                    out=acc[:],
                    lhsT=hc[i][:, P * g : P * (g + 1)].bitcast(FP8X4),
                    lhsT_scale=hs[i][:, P * g : P * (g + 1)],
                    rhs=w2c[:, o : o + N].bitcast(FP8X4),
                    rhs_scale=w2s[:, o : o + N],
                    start=(g == 0),
                    stop=(g == KP - 1),
                )

        def V1(i):
            mu[i] = work.tile([P, N], F32, name="mu", tag="mu", bufs=MUB)
            nc.vector.tensor_tensor(out=mu[i][:], in0=fmu[i][:], in1=bias[:, 0:N], op=ALU.add)

        def MB(i):
            if i in CAST:
                mub[i] = work.tile([P, N], BF16, name="mub", tag="mub", bufs=2, align_bytes=64)
                nc.vector.tensor_copy(out=mub[i][:], in_=mu[i][:])

        def V2(i):
            lv[i] = work.tile([P, N], F32, name="lv", tag="lv", bufs=2)
            nc.vector.scalar_tensor_tensor(
                out=lv[i][:], in0=flv[i][:], scalar=1.0, in1=bias[:, N : 2 * N], op0=ALU.mult, op1=ALU.add, accum_out=slv[:, i : i + 1]
            )

        def TM(i):
            mt[i] = psum.tile([P, 4, P], F32, name="mt", tag="mt", bufs=1)
            if i in CAST:
                mw = mub[i][:].bitcast(F32)
                for u in range(2):
                    nc.tensor.transpose(mt[i][:, u, :], mw[:, P * u : P * (u + 1)], ident[:])
            else:
                for t in range(4):
                    o = 256 * (t // 2) + t % 2
                    nc.tensor.transpose(mt[i][:, t, :], mu[i][:, P * t : P * (t + 1)] if PERM else mu[i][:, o : o + 255 : 2], ident[:])

        def CM(i):
            mg[i] = work.tile([P, N], BF16, name="mg", tag="mg", bufs=2, align_bytes=64)
            if i in CAST:
                nc.scalar.copy(out=mg[i][:].bitcast(F32).rearrange("p (r u) -> p r u", u=2), in_=mt[i][:, 0:2, :].rearrange("p u r -> p r u"))
            else:
                nc.scalar.copy(out=mg[i][:].rearrange("p (r t) -> p r t", t=4), in_=mt[i][:].rearrange("p t r -> p r t"))

        def QM(i):
            mc[i] = work.tile([P, P], U32, name="mc", tag="mc", bufs=2, align_bytes=64)
            ms[i] = work.tile([P, P], U8, name="ms", tag="ms", bufs=2, align_bytes=64)
            quant(mg[i], mc[i][:], ms[i][:])

        def MU(i):
            ub[i] = psum.tile([P, N], F32, name="u", tag="u", bufs=2)
            nc.tensor.matmul_mx(
                out=ub[i][:],
                lhsT=mc[i][:].bitcast(FP8X4),
                lhsT_scale=ms[i][:],
                rhs=wvc[:].bitcast(FP8X4),
                rhs_scale=wvs[:],
                start=True,
                stop=True,
            )

        def SU(i):
            square_sum(ub[i][:], ssm[:, i : i + 1])

        def SD(i):
            std[i] = work.tile([P, N], F32, name="std", tag="std", bufs=STB)
            nc.scalar.activation(out=std[i][:], in_=lv[i][:], func=ACT.Exp, scale=0.5)

        def SI(i):
            istd[i] = work.tile([P, N], F32, name="istd", tag="istd", bufs=ISB)
            nc.scalar.activation(out=istd[i][:], in_=lv[i][:], func=ACT.Exp, scale=-0.5)

        def VT(i):
            tt[i] = work.tile([P, N], F32, name="tt", tag="tt", bufs=TTB)
            eng = nc.vector if i in VT_V else nc.gpsimd
            eng.tensor_tensor(out=tt[i][:], in0=std[i][:], in1=eraw[i // 4][:, N * (i % 4) : N * (i % 4 + 1)], op=ALU.mult)

        def T1(i):
            sm[i] = work.tile([P, 4], F32, name="sm", tag="sm", bufs=4)
            (nc.gpsimd if T_G else nc.vector).tensor_scalar(
                out=sm[i][:, 0:1], in0=ssm[:, i : i + 1], scalar1=1e-3, scalar2=bvx[:, i : i + 1], op0=ALU.add, op1=ALU.max
            )

        def T2(i):
            if T_G:
                nc.gpsimd.tensor_tensor(out=sm[i][:, 1:2], in0=sm[i][:, 0:1], in1=neg[:], op=ALU.pow)
            else:
                nc.vector.reciprocal(out=sm[i][:, 1:2], in_=sm[i][:, 0:1])

        def T3(i, on_s=False):
            if T_G:
                nc.gpsimd.tensor_tensor(out=sm[i][:, 2:3], in0=sm[i][:, 1:2], in1=bvx[:, i : i + 1], op=ALU.mult)
            else:
                if on_s:
                    nc.scalar.activation(out=sm[i][:, 2:3], in_=sm[i][:, 1:2], func=ACT.Copy, scale=bvx[:, i : i + 1])
                else:
                    nc.vector.tensor_scalar(out=sm[i][:, 2:3], in0=sm[i][:, 1:2], scalar1=bvx[:, i : i + 1], scalar2=None, op0=ALU.mult)

        def TP1(i):
            sm[i] = work.tile([P, 8], F32, name="sm", tag="sm", bufs=3)
            nc.vector.scalar_tensor_tensor(
                out=sm[i][:, 0:2], in0=ssm[:, i : i + 2], scalar=1e-3, in1=bvx[:, i : i + 2], op0=ALU.add, op1=ALU.max
            )

        def TP2(i):
            nc.vector.reciprocal(out=sm[i][:, 2:4], in_=sm[i][:, 0:2])

        def TP3(i):
            nc.vector.tensor_tensor(out=sm[i][:, 4:6], in0=sm[i][:, 2:4], in1=bvx[:, i : i + 2], op=ALU.mult)

        def SC(i):
            if TP:
                return sm[i - i % 2][:, 4 + i % 2 : 5 + i % 2]
            return sm[i][:, 2:3]

        def ND(i):
            nd[i] = work.tile([P, N], F32, name="nd", tag="nd", bufs=NDB)
            nc.vector.scalar_tensor_tensor(
                out=nd[i][:], in0=mu[i][:], scalar=SC(i), in1=yraw[i // 4][:, N * (i % 4) : N * (i % 4 + 1)], op0=ALU.mult, op1=ALU.subtract
            )

        def FX(i):
            fx = work.tile([P, N], F32, name="fx", tag="fx", bufs=2)
            nc.vector.scalar_tensor_tensor(out=fx[:], in0=mu[i][:], scalar=SC(i), in1=tt[i][:], op0=ALU.mult, op1=ALU.add)
            nc.sync.dma_start(out=fx_v[:, i, :], in_=fx[:])

        def EE(i):
            ee[i] = work.tile([P, N], F32, name="ee", tag="ee", bufs=2)
            (nc.gpsimd if i in EE_G else nc.vector).tensor_tensor(out=ee[i][:], in0=nd[i][:], in1=istd[i][:], op=ALU.mult)

        def SQ(i):
            square_sum(ee[i][:], ssq[:, i : i + 1])

        def XX(j, tags=("f", "f", "f", "f")):
            for i in range(4 * j, 4 * j + 4):
                XS(i, XM(i, "f", 3))

        EXU = {}
        EXP = {}
        brow = keep.tile([P, 2 * N], BF16, name="brow", tag="brow")
        ones = keep.tile([P, P], BF16, name="ones", tag="ones")
        nc.gpsimd.memset(brow[:], 0.0)
        nc.gpsimd.memset(ones[:], 1.0)
        nc.vector.memset(neg[:], -1.0)
        def load_hh(i):
            if i % 2 == 0:
                hraw[i // 2] = work.tile([P, 2 * H], BF16, name="hraw", tag="hraw", bufs=4)
            nc.sync.dma_start(out=hraw[i // 2][:, H * (i % 2) : H * (i % 2 + 1)], in_=h_v[:, i, :])
        load_x(0, 0, 2)
        load_wv()
        load_x(0, 2, 4)
        nc.sync.dma_start(out=brow[0:1, :], in_=b2.rearrange("(o n) -> o n", o=1))
        load_w2(0)
        load_x(1)
        load_w2(1)
        load_x(2)
        load_w2(2)
        load_hh(0)
        load_x(3)
        XT(0, 0)
        XT(0, 1)
        VR()
        VQ()
        XQ(0)
        for half in range(2):
            b_ps = psum.tile([P, N], F32, name="u", tag="u", bufs=2)
            nc.tensor.matmul(out=b_ps[:], lhsT=ones[:], rhs=brow[:, N * half : N * (half + 1)], start=True, stop=True)
            nc.scalar.copy(out=bias[:, N * half : N * (half + 1)], in_=b_ps[:])
        WR(0, 0)
        XT(1, 0)
        XT(1, 1)
        XX(0)
        WR(0, 1)
        WQ(0, 0)
        WQ(0, 1)
        load_w2(3)
        load_hh(1)
        load_h(1)
        load_ye(0)
        XQ(1)
        XT(2, 0)
        XT(2, 1)
        XX(1)
        WR(1, 0)
        WR(1, 1)
        WQ(1, 0)
        WQ(1, 1)
        XQ(2)
        TH(0)
        CH(0, 0)
        CH(0, 1)
        WR(2, 0)
        XT(3, 0)
        XT(3, 1)
        WR(2, 1)
        WQ(2, 0)
        WQ(2, 1)
        XX(2)
        TH(1)
        CH(1, 0)
        CH(1, 1)
        QH(0)
        WR(3, 0)
        WQ(3, 0)
        EXTRA = {-2: (lambda: load_h(2),lambda: load_ye(1)), -1: (lambda: load_h(3),)}
        EXU = {-1: (lambda: WQ(3, 1),), 0: (lambda: XQ(3),)}
        EXV = {-2: (lambda: WR(3, 1),), 0: (lambda: XBS(0, 3),), 9: (lambda: XBS(3),)}
        XSTEP = {2: (12,), 4: (13,), 6: (14,), 8: (15,)}
        ux = {}
        def ok(i):
            return 0 <= i < NT
        for a in range(-2, NT + 1):
            for f in EXTRA.get(a, ()):
                f()
            if (a + LD) % 2 == 0 and HLD < (a + LD) // 2 < NT // 2:
                load_h((a + LD) // 2)
            if a == 2:
                load_ye(2)
            if a == 6:
                load_ye(3)
            if ok(a):
                CM(a)
            if ok(a + 3) and a + 3 > CH0:
                CH(a + 3, 0)
                CH(a + 3, 1)
            if ok(a + 1):
                V1(a + 1)
            if ok(a - 1):
                T1(a - 1)
            for f in EXU.get(a, ()):
                f()
            if ok(a):
                V2(a)
            if ok(a - 1):
                VT(a - 1)
                T2(a - 1)
            if ok(a + 1):
                MB(a + 1)
            if ok(a):
                QM(a)
            for f in EXV.get(a, ()):
                f()
            if ok(a - 1):
                T3(a - 1)
            if ok(a - 2):
                EE(a - 2)
            if ok(a + 2):
                MF(a + 2, 0)
            for f in EXP.get(a, ()):
                f()
            if MUF and ok(a):
                MU(a)
            if ok(a + 1):
                MF(a + 1, 1)
            if not MUF and ok(a):
                MU(a)
            for k in XSTEP.get(a, ()):
                ux[k] = XM(k, "u", 2)
            if ok(a + 1):
                TM(a + 1)
            if ok(a + 4) and a + 4 > TH0:
                TH(a + 4)
            if ok(a):
                SD(a)
                SI(a)
                SU(a)
            if ok(a - 2):
                SQ(a - 2)
            for k in XSTEP.get(a, ()):
                XS(k, ux[k])
            if ok(a - 1):
                ND(a - 1)
            if a == NT:
                EE(a - 1)
                SQ(a - 1)
            if ok(a - 1):
                FX(a - 1)
            if ok(a + 3) and a + 3 > QH0:
                QH(a + 3)
        nc.vector.tensor_scalar(
            out=lpc[:], in0=slv[:], scalar1=-0.5, scalar2=-0.5 * N * math.log(2.0 * math.pi), op0=ALU.mult, op1=ALU.add
        )
        nc.vector.scalar_tensor_tensor(out=lp[:], in0=ssq[:], scalar=-0.5, in1=lpc[:], op0=ALU.mult, op1=ALU.add)
        nc.sync.dma_start(out=lp_v, in_=lp[:])
